import numpy as np
import ml_dtypes


def mxq(x, axis, fmt="e4m3"):
    dtype, down = {"e4m3": (ml_dtypes.float8_e4m3fn, 7), "e5m2": (ml_dtypes.float8_e5m2, 14)}[fmt]
    v = np.moveaxis(np.asarray(x, np.float32).astype(ml_dtypes.bfloat16).astype(np.float64), axis, -1)
    blocks = v.reshape(v.shape[:-1] + (-1, 32))
    amax = np.abs(blocks).max(-1, keepdims=True)
    byte = np.maximum(np.where(amax > 0, np.frexp(amax)[1] - 1 + 127, 0) - down, 1)
    scale = np.exp2(byte - 127.0)
    codes = (blocks / scale).astype(np.float32).astype(dtype).astype(np.float64)
    return np.moveaxis((codes * scale).reshape(v.shape), -1, axis)


WIDE = False


def mx_kscale(k):
    if not WIDE:
        return np.ones(k)
    levels = np.array([10, -10, 5, -5, 0])
    if k % 512:
        return np.exp2(np.random.permutation(np.resize(levels, k // 32))).repeat(32)
    a = np.empty((k // 512, 16))
    for p in range(k // 512):
        a[p, :8] = np.random.permutation(np.resize(levels, 8))
        for g in range(8):
            far = levels[np.abs(levels - a[p, g]) >= 10]
            a[p, g + 8] = far[np.random.randint(len(far))]
    return np.exp2(a.ravel()).repeat(32)


BF16 = ml_dtypes.bfloat16


def bf(x):
    return np.asarray(x, np.float32).astype(BF16)


def f64(x):
    return np.asarray(x).astype(np.float64)


N, C, T, V, S, INTER = 4, 1024, 32, 128, 4, 32
KT = INTER * T


def setup_inputs():
    s = mx_kscale(C)
    u = mx_kscale(KT)[::T]
    g = np.sqrt(1.5) * KT ** 0.25 / np.sqrt(C)
    mu = 0.25 * np.random.standard_normal((1, C, 1, 1))
    return {'x': bf((np.random.standard_normal((N, C, T, V)) + mu) * s[None, :, None, None]),
            'A': bf(2.0 * np.random.random((S, V, V)) / V),
            'PA': bf(np.random.standard_normal((S, V, V)) / V),
            'Wa': bf(np.random.standard_normal((S, INTER, C)) * g * u[None, :, None] / s[None, None, :]),
            'Wb': bf(np.random.standard_normal((S, INTER, C)) * g / u[None, :, None] / s[None, None, :])}


def reference(x, A, PA, Wa, Wb):
    xq = mxq(f64(x).reshape(N, C, T * V), 1, 'e4m3')
    fa = (mxq(f64(Wa).reshape(S * INTER, C), 1, 'e4m3') @ xq).reshape(N, S, KT, V)
    fb = (mxq(f64(Wb).reshape(S * INTER, C), 1, 'e4m3') @ xq).reshape(N, S, KT, V)
    scores = (np.swapaxes(mxq(fa, 2, 'e4m3'), -1, -2) @ mxq(fb, 2, 'e4m3')) / KT
    e = np.exp(scores - scores.max(-2, keepdims=True))
    attn = e / e.sum(-2, keepdims=True)
    return attn + (f64(A) + f64(PA))[None]

@@ -1,0 +1,253 @@
+from contextlib import ExitStack
+
+import concourse.mybir as mybir
+from concourse.masks import make_identity
+
+F32 = mybir.dt.float32
+BF16 = mybir.dt.bfloat16
+U32 = mybir.dt.uint32
+U8 = mybir.dt.uint8
+FP8X4 = mybir.dt.float8_e4m3fn_x4
+ALU = mybir.AluOpType
+ACT = mybir.ActivationFunctionType
+
+N, C, T, V, S, INTER = 4, 1024, 32, 128, 4, 32
+KT = INTER * T
+
+P = 128
+PACK = 4
+K_PASS = P * PACK
+C_PASSES = C // K_PASS
+
+SIDES = 2
+W_ROWS = SIDES * S * INTER
+OPERANDS = SIDES * S
+FRAME_WORDS = T // PACK
+PAIR = 2
+PAIRS = PACK // PAIR
+
+GROUPS = KT // K_PASS
+GROUP_FRAMES = T // GROUPS
+GROUP_COLS = GROUP_FRAMES * V
+CHUNK_COLS = 1024
+GROUP_CHUNKS = C_PASSES * GROUP_COLS // CHUNK_COLS
+SCALAR_CHUNKS, OF_CHUNKS = 5, 16
+SAMPLES_BEHIND = 1
+BANK_FRAMES = PAIR
+BANK_OPERANDS = 2
+
+FLOPS = 2 * W_ROWS * C * N * T * V + 2 * N * S * V * V * KT
+
+
+def quantise_weights(nc, consts, psum_flip, ident, Wa, Wb):
+    w_rows = consts.tile([P, SIDES * C], BF16)
+    nc.scalar.dma_start(out=w_rows[:, 0:C], in_=Wa.rearrange("s i c -> (s i) c"))
+    nc.scalar.dma_start(out=w_rows[:, C : 2 * C], in_=Wb.rearrange("s i c -> (s i) c"))
+    w_words = w_rows[:].bitcast(F32)
+    pair_words = C // 2
+
+    w_grouped = consts.tile([P, C_PASSES * W_ROWS * PACK], BF16, align_bytes=64)
+    w_grouped_words = w_grouped[:].bitcast(F32).rearrange(
+        "p (h i a s u) -> p h a u s i", h=C_PASSES, i=INTER, a=SIDES, s=S, u=PAIRS
+    )
+    for h in range(C_PASSES):
+        w_flipped = psum_flip.tile([P, SIDES, 2, P], F32, tag="flipped")
+        for a in range(SIDES):
+            for u in range(2):
+                first = a * pair_words + h * (K_PASS // 2) + u
+                nc.tensor.transpose(
+                    w_flipped[:, a, u, :], w_words[:, first : first + K_PASS // 2 - 1 : 2], ident[:]
+                )
+        for a in range(SIDES):
+            for u in range(2):
+                nc.vector.tensor_copy(
+                    out=w_grouped_words[:, h, a, u],
+                    in_=w_flipped[:, a, u, :].rearrange("p (s i) -> p s i", s=S),
+                )
+    w_codes = consts.tile([P, C_PASSES, W_ROWS], U32, align_bytes=64)
+    w_scales = consts.tile([P, C_PASSES, W_ROWS], U8, align_bytes=64)
+    nc.vector.quantize_mx(
+        out=w_codes[:].rearrange("p h r -> p (h r)").bitcast(FP8X4),
+        scales=w_scales[:].rearrange("p h r -> p (h r)"),
+        in_=w_grouped[:],
+    )
+    return w_codes, w_scales
+
+
+def regroup_x_chunk(copy, grouped_pool, raw):
+    grouped = grouped_pool.tile([P, CHUNK_COLS * PACK], BF16, align_bytes=64)
+    copy(
+        out=grouped[:].rearrange("p (c i j) -> p c j i", i=4, j=PACK),
+        in_=raw[:].rearrange("p j (c i) -> p c j i", i=4),
+    )
+    return grouped
+
+
+def tile_unitagcn_pa_t_kernel(tc, x, A, PA, Wa, Wb, out):
+    nc = tc.nc
+    with ExitStack() as stack:
+        consts = stack.enter_context(tc.tile_pool(name="consts", bufs=1))
+        raw_pool = stack.enter_context(tc.tile_pool(name="raw", bufs=6))
+        grouped_pool = stack.enter_context(tc.tile_pool(name="grouped", bufs=4))
+        xq_pool = stack.enter_context(tc.tile_pool(name="xq", bufs=2))
+        rows_pool = stack.enter_context(
+            tc.tile_pool(name="rows", bufs=SAMPLES_BEHIND + 1)
+        )
+        f_pool = stack.enter_context(tc.tile_pool(name="f", bufs=2))
+        soft_pool = stack.enter_context(tc.tile_pool(name="soft", bufs=2))
+        psum_proj = stack.enter_context(tc.psum_pool(name="psum_proj", bufs=4))
+        psum_flip = stack.enter_context(tc.psum_pool(name="psum_flip", bufs=2))
+        psum_score = stack.enter_context(tc.psum_pool(name="psum_score", bufs=1))
+
+        ident = consts.tile([P, P], F32)
+        make_identity(nc, ident[:])
+        w_codes, w_scales = quantise_weights(nc, consts, psum_flip, ident, Wa, Wb)
+
+        a_rows = consts.tile([P, S, V], BF16)
+        pa_rows = consts.tile([P, S, V], BF16)
+        nc.scalar.dma_start(out=a_rows[:], in_=A.rearrange("s v w -> v s w"))
+        nc.scalar.dma_start(out=pa_rows[:], in_=PA.rearrange("s v w -> v s w"))
+        adjacency = consts.tile([P, S, V], F32)
+        nc.gpsimd.tensor_tensor(out=adjacency[:], in0=a_rows[:], in1=pa_rows[:], op=ALU.add)
+
+        def project_group(n, g, f_rows):
+            x_rows = x[n].rearrange("(h p j) t v -> h p j (t v)", h=C_PASSES, p=P, j=PACK)
+            x_codes = xq_pool.tile([P, C_PASSES, GROUP_COLS], U32, align_bytes=64)
+            x_scales = xq_pool.tile([P, C_PASSES, GROUP_COLS], U8, align_bytes=64)
+            waiting = None
+            for chunk in range(GROUP_CHUNKS + 1):
+                regrouped = None
+                if chunk < GROUP_CHUNKS:
+                    half, h = divmod(chunk, C_PASSES)
+                    cols = slice(half * CHUNK_COLS, (half + 1) * CHUNK_COLS)
+                    first_col = g * GROUP_COLS + half * CHUNK_COLS
+                    raw = raw_pool.tile([P, PACK, CHUNK_COLS], BF16)
+                    nc.sync.dma_start(
+                        out=raw[:], in_=x_rows[h][:, :, first_col : first_col + CHUNK_COLS]
+                    )
+                    count = 3 + (n * GROUPS + g) * GROUP_CHUNKS + chunk
+                    on_scalar = (count * SCALAR_CHUNKS) % OF_CHUNKS < SCALAR_CHUNKS
+                    regrouped = (
+                        regroup_x_chunk(
+                            nc.scalar.copy if on_scalar else nc.vector.tensor_copy, grouped_pool, raw
+                        ),
+                        x_codes[:, h, cols],
+                        x_scales[:, h, cols],
+                    )
+                if waiting is not None:
+                    nc.vector.quantize_mx(
+                        out=waiting[1].bitcast(FP8X4), scales=waiting[2], in_=waiting[0][:]
+                    )
+                waiting = regrouped
+
+            f_rows_view = f_rows[:].rearrange(
+                "p (u i t q e) -> p t u i q e", u=PAIRS, i=INTER, t=FRAME_WORDS, q=OPERANDS, e=PAIR
+            )
+            for first_frame in range(0, GROUP_FRAMES, BANK_FRAMES):
+                proj = psum_proj.tile([P, BANK_FRAMES, W_ROWS], F32)
+                for f in range(BANK_FRAMES):
+                    joints = slice((first_frame + f) * V, (first_frame + f + 1) * V)
+                    for h in range(C_PASSES):
+                        nc.tensor.matmul_mx(
+                            out=proj[:, f, :],
+                            lhsT=x_codes[:, h, joints].bitcast(FP8X4),
+                            lhsT_scale=x_scales[:, h, joints],
+                            rhs=w_codes[:, h, :].bitcast(FP8X4),
+                            rhs_scale=w_scales[:, h, :],
+                            start=(h == 0),
+                            stop=(h == C_PASSES - 1),
+                        )
+                t_word, u = divmod((g * GROUP_FRAMES + first_frame) // PAIR, PAIRS)
+                nc.scalar.copy(
+                    out=f_rows_view[:, t_word, u],
+                    in_=proj[:].rearrange("p e (i q) -> p i q e", q=OPERANDS),
+                )
+
+        def quantise_pass(f_rows, g, codes, scales):
+            f_words = f_rows[:].bitcast(F32)
+            plane_words = INTER * FRAME_WORDS * OPERANDS
+            pass_words = P * OPERANDS
+            f_grouped = f_pool.tile([P, OPERANDS * V * PACK], BF16, align_bytes=64)
+            f_grouped_words = f_grouped[:].bitcast(F32).rearrange(
+                "p (o v u) -> p o v u", o=OPERANDS, v=V, u=2
+            )
+            for first_operand in range(0, OPERANDS, BANK_OPERANDS):
+                flipped = psum_flip.tile([P, BANK_OPERANDS, 2, V], F32, tag="flipped")
+                for o in range(BANK_OPERANDS):
+                    for u in range(2):
+                        first = u * plane_words + g * pass_words + first_operand + o
+                        nc.tensor.transpose(
+                            flipped[:, o, u, :],
+                            f_words[:, first : first + pass_words - OPERANDS + 1 : OPERANDS],
+                            ident[:],
+                        )
+                nc.scalar.copy(
+                    out=f_grouped_words[:, first_operand : first_operand + BANK_OPERANDS],
+                    in_=flipped[:].rearrange("p o u v -> p o v u"),
+                )
+            nc.vector.quantize_mx(out=codes.bitcast(FP8X4), scales=scales, in_=f_grouped[:])
+
+        def attend(n, f_rows):
+            f_codes = f_pool.tile([P, GROUPS, OPERANDS * V], U32, align_bytes=64)
+            f_scales = f_pool.tile([P, GROUPS, OPERANDS * V], U8, align_bytes=64)
+            for g in range(GROUPS):
+                quantise_pass(f_rows, g, f_codes[:, g, :], f_scales[:, g, :])
+
+            scores = psum_score.tile([P, S, V], F32)
+            for s in range(S):
+                fa_cols = slice(s * V, (s + 1) * V)
+                fb_cols = slice((S + s) * V, (S + s + 1) * V)
+                for g in range(GROUPS):
+                    nc.tensor.matmul_mx(
+                        out=scores[:, s, :],
+                        lhsT=f_codes[:, g, fb_cols].bitcast(FP8X4),
+                        lhsT_scale=f_scales[:, g, fb_cols],
+                        rhs=f_codes[:, g, fa_cols].bitcast(FP8X4),
+                        rhs_scale=f_scales[:, g, fa_cols],
+                        start=(g == 0),
+                        stop=(g == GROUPS - 1),
+                    )
+
+            top = soft_pool.tile([P, S], F32)
+            nc.vector.tensor_reduce(out=top[:], in_=scores[:], axis=mybir.AxisListType.X, op=ALU.max)
+            shift = soft_pool.tile([P, S], F32)
+            nc.vector.tensor_scalar(
+                out=shift[:], in0=top[:], scalar1=-1.0 / KT, scalar2=None, op0=ALU.mult
+            )
+            expd = soft_pool.tile([P, S, V], F32)
+            sums = soft_pool.tile([P, S], F32)
+            for s in range(S):
+                nc.scalar.activation(
+                    out=expd[:, s, :],
+                    in_=scores[:, s, :],
+                    func=ACT.Exp,
+                    bias=shift[:, s : s + 1],
+                    scale=1.0 / KT,
+                    accum_out=sums[:, s : s + 1],
+                )
+            inverse = soft_pool.tile([P, S], F32)
+            nc.vector.reciprocal(out=inverse[:], in_=sums[:])
+            attn = soft_pool.tile([P, S, V], F32)
+            nc.vector.tensor_tensor(
+                out=attn[:],
+                in0=expd[:],
+                in1=inverse[:].unsqueeze(2).to_broadcast([P, S, V]),
+                op=ALU.mult,
+            )
+
+            attn_flipped = psum_score.tile([P, S, V], F32)
+            for s in range(S):
+                nc.tensor.transpose(attn_flipped[:, s, :], attn[:, s, :], ident[:])
+            result = soft_pool.tile([P, S, V], F32)
+            nc.vector.tensor_tensor(out=result[:], in0=attn_flipped[:], in1=adjacency[:], op=ALU.add)
+            nc.sync.dma_start(out=out[n].rearrange("s v w -> v s w"), in_=result[:])
+
+        projected = {}
+        for n in range(N + SAMPLES_BEHIND):
+            if n < N:
+                f_rows = rows_pool.tile([P, T * W_ROWS], BF16)
+                for g in range(GROUPS):
+                    project_group(n, g, f_rows)
+                projected[n] = f_rows
+            if n >= SAMPLES_BEHIND:
+                attend(n - SAMPLES_BEHIND, projected[n - SAMPLES_BEHIND])

@@ -16,238 +16,319 @@ KT = INTER * T
 
 P = 128
 PACK = 4
+PAIRS = PACK // 2
 K_PASS = P * PACK
 C_PASSES = C // K_PASS
+KT_PASSES = KT // K_PASS
+HALF = INTER // KT_PASSES
 
 SIDES = 2
-W_ROWS = SIDES * S * INTER
+SIDE_ROWS = S * INTER
 OPERANDS = SIDES * S
-FRAME_WORDS = T // PACK
-PAIR = 2
-PAIRS = PACK // PAIR
+WORDS = T // PACK
 
-GROUPS = KT // K_PASS
-GROUP_FRAMES = T // GROUPS
-GROUP_COLS = GROUP_FRAMES * V
-CHUNK_COLS = 1024
-GROUP_CHUNKS = C_PASSES * GROUP_COLS // CHUNK_COLS
-SCALAR_CHUNKS, OF_CHUNKS = 5, 16
-SAMPLES_BEHIND = 1
-BANK_FRAMES = PAIR
-BANK_OPERANDS = 2
+BLOCK = 1024
+BLOCKS = T * V // BLOCK
+RUN = PACK * V
+RUNS = BLOCK // RUN
+STEPS = N * BLOCKS
+AHEAD = 2
+FIRST_PIECE = BLOCK // 4
+SCALAR_COLS = 896
 
-FLOPS = 2 * W_ROWS * C * N * T * V + 2 * N * S * V * V * KT
-
-
-def quantise_weights(nc, consts, psum_flip, ident, Wa, Wb):
-    w_rows = consts.tile([P, SIDES * C], BF16)
-    nc.scalar.dma_start(out=w_rows[:, 0:C], in_=Wa.rearrange("s i c -> (s i) c"))
-    nc.scalar.dma_start(out=w_rows[:, C : 2 * C], in_=Wb.rearrange("s i c -> (s i) c"))
-    w_words = w_rows[:].bitcast(F32)
-    pair_words = C // 2
-
-    w_grouped = consts.tile([P, C_PASSES * W_ROWS * PACK], BF16, align_bytes=64)
-    w_grouped_words = w_grouped[:].bitcast(F32).rearrange(
-        "p (h i a s u) -> p h a u s i", h=C_PASSES, i=INTER, a=SIDES, s=S, u=PAIRS
-    )
-    for h in range(C_PASSES):
-        w_flipped = psum_flip.tile([P, SIDES, 2, P], F32, tag="flipped")
-        for a in range(SIDES):
-            for u in range(2):
-                first = a * pair_words + h * (K_PASS // 2) + u
-                nc.tensor.transpose(
-                    w_flipped[:, a, u, :], w_words[:, first : first + K_PASS // 2 - 1 : 2], ident[:]
-                )
-        for a in range(SIDES):
-            for u in range(2):
-                nc.vector.tensor_copy(
-                    out=w_grouped_words[:, h, a, u],
-                    in_=w_flipped[:, a, u, :].rearrange("p (s i) -> p s i", s=S),
-                )
-    w_codes = consts.tile([P, C_PASSES, W_ROWS], U32, align_bytes=64)
-    w_scales = consts.tile([P, C_PASSES, W_ROWS], U8, align_bytes=64)
-    nc.vector.quantize_mx(
-        out=w_codes[:].rearrange("p h r -> p (h r)").bitcast(FP8X4),
-        scales=w_scales[:].rearrange("p h r -> p (h r)"),
-        in_=w_grouped[:],
-    )
-    return w_codes, w_scales
-
-
-def regroup_x_chunk(copy, grouped_pool, raw):
-    grouped = grouped_pool.tile([P, CHUNK_COLS * PACK], BF16, align_bytes=64)
-    copy(
-        out=grouped[:].rearrange("p (c i j) -> p c j i", i=4, j=PACK),
-        in_=raw[:].rearrange("p j (c i) -> p c j i", i=4),
-    )
-    return grouped
+FLOPS = 2 * SIDES * SIDE_ROWS * C * N * T * V + 2 * N * S * V * V * KT
 
 
 def tile_unitagcn_pa_t_kernel(tc, x, A, PA, Wa, Wb, out):
     nc = tc.nc
     with ExitStack() as stack:
         consts = stack.enter_context(tc.tile_pool(name="consts", bufs=1))
-        raw_pool = stack.enter_context(tc.tile_pool(name="raw", bufs=6))
+        raw_pool = stack.enter_context(tc.tile_pool(name="raw", bufs=C_PASSES * (AHEAD + 1)))
         grouped_pool = stack.enter_context(tc.tile_pool(name="grouped", bufs=4))
-        xq_pool = stack.enter_context(tc.tile_pool(name="xq", bufs=2))
-        rows_pool = stack.enter_context(
-            tc.tile_pool(name="rows", bufs=SAMPLES_BEHIND + 1)
-        )
+        xq_pool = stack.enter_context(tc.tile_pool(name="xq", bufs=3))
+        rows_pool = stack.enter_context(tc.tile_pool(name="rows", bufs=4))
         f_pool = stack.enter_context(tc.tile_pool(name="f", bufs=2))
         soft_pool = stack.enter_context(tc.tile_pool(name="soft", bufs=2))
-        psum_proj = stack.enter_context(tc.psum_pool(name="psum_proj", bufs=4))
-        psum_flip = stack.enter_context(tc.psum_pool(name="psum_flip", bufs=2))
+        psum_proj = stack.enter_context(tc.psum_pool(name="psum_proj", bufs=6))
         psum_score = stack.enter_context(tc.psum_pool(name="psum_score", bufs=1))
+        stack.enter_context(tc.manual_schedule())
 
-        ident = consts.tile([P, P], F32)
-        make_identity(nc, ident[:])
-        w_codes, w_scales = quantise_weights(nc, consts, psum_flip, ident, Wa, Wb)
+        raws = {}
 
+        def load(k, pieces=1):
+            n, part = divmod(k, BLOCKS)
+            x_rows = x[n].rearrange("(h p j) t v -> h p j (t v)", h=C_PASSES, p=P, j=PACK)
+            raws[k] = []
+            for h in range(C_PASSES):
+                raw = raw_pool.tile([P, PACK, BLOCK], BF16)
+                width = BLOCK // pieces
+                for first in range(0, BLOCK, width):
+                    column = part * BLOCK + first
+                    nc.sync.dma_start(
+                        out=raw[:, :, first : first + width],
+                        in_=x_rows[h][:, :, column : column + width],
+                    )
+                raws[k].append(raw)
+
+        w_rows = consts.tile([P, SIDES * C], BF16)
+        nc.scalar.dma_start(out=w_rows[:, 0:C], in_=Wa.rearrange("s i c -> (s i) c"))
+        nc.scalar.dma_start(out=w_rows[:, C : 2 * C], in_=Wb.rearrange("s i c -> (s i) c"))
+        load(0, pieces=BLOCK // FIRST_PIECE)
+        for k in range(1, AHEAD):
+            load(k)
         a_rows = consts.tile([P, S, V], BF16)
         pa_rows = consts.tile([P, S, V], BF16)
         nc.scalar.dma_start(out=a_rows[:], in_=A.rearrange("s v w -> v s w"))
         nc.scalar.dma_start(out=pa_rows[:], in_=PA.rearrange("s v w -> v s w"))
+
+        ident = consts.tile([P, P], F32)
+        make_identity(nc, ident[:])
         adjacency = consts.tile([P, S, V], F32)
         nc.gpsimd.tensor_tensor(out=adjacency[:], in0=a_rows[:], in1=pa_rows[:], op=ALU.add)
 
-        def project_group(n, g, f_rows):
-            x_rows = x[n].rearrange("(h p j) t v -> h p j (t v)", h=C_PASSES, p=P, j=PACK)
-            x_codes = xq_pool.tile([P, C_PASSES, GROUP_COLS], U32, align_bytes=64)
-            x_scales = xq_pool.tile([P, C_PASSES, GROUP_COLS], U8, align_bytes=64)
-            waiting = None
-            for chunk in range(GROUP_CHUNKS + 1):
-                regrouped = None
-                if chunk < GROUP_CHUNKS:
-                    half, h = divmod(chunk, C_PASSES)
-                    cols = slice(half * CHUNK_COLS, (half + 1) * CHUNK_COLS)
-                    first_col = g * GROUP_COLS + half * CHUNK_COLS
-                    raw = raw_pool.tile([P, PACK, CHUNK_COLS], BF16)
-                    nc.sync.dma_start(
-                        out=raw[:], in_=x_rows[h][:, :, first_col : first_col + CHUNK_COLS]
+        w_words = w_rows[:].bitcast(F32).rearrange("p (a c) -> p a c", a=SIDES)
+        w_grouped = consts.tile([P, C_PASSES * SIDES * SIDE_ROWS * PACK], BF16, align_bytes=64)
+        w_grouped_words = w_grouped[:].bitcast(F32).rearrange(
+            "p (h a i b s u) -> p h a b i s u",
+            h=C_PASSES, a=SIDES, i=HALF, b=KT_PASSES, s=S, u=PAIRS,
+        )
+        w_codes = consts.tile([P, C_PASSES, SIDES * SIDE_ROWS], U32, align_bytes=64)
+        w_scales = consts.tile([P, C_PASSES, SIDES * SIDE_ROWS], U8, align_bytes=64)
+        for h in range(C_PASSES):
+            w_flipped = psum_proj.tile([P, SIDES, PAIRS, SIDE_ROWS], F32, tag="bank")
+            for a in range(SIDES):
+                for u in range(PAIRS):
+                    first = h * (K_PASS // 2) + u
+                    nc.tensor.transpose(
+                        w_flipped[:, a, u, :],
+                        w_words[:, a, first : first + K_PASS // 2 - 1 : PAIRS],
+                        ident[:],
                     )
-                    count = 3 + (n * GROUPS + g) * GROUP_CHUNKS + chunk
-                    on_scalar = (count * SCALAR_CHUNKS) % OF_CHUNKS < SCALAR_CHUNKS
-                    regrouped = (
-                        regroup_x_chunk(
-                            nc.scalar.copy if on_scalar else nc.vector.tensor_copy, grouped_pool, raw
-                        ),
-                        x_codes[:, h, cols],
-                        x_scales[:, h, cols],
-                    )
-                if waiting is not None:
-                    nc.vector.quantize_mx(
-                        out=waiting[1].bitcast(FP8X4), scales=waiting[2], in_=waiting[0][:]
-                    )
-                waiting = regrouped
-
-            f_rows_view = f_rows[:].rearrange(
-                "p (u i t q e) -> p t u i q e", u=PAIRS, i=INTER, t=FRAME_WORDS, q=OPERANDS, e=PAIR
+            w_flipped_rows = w_flipped[:].rearrange(
+                "p a u (s b i) -> p a b i s u", s=S, b=KT_PASSES
             )
-            for first_frame in range(0, GROUP_FRAMES, BANK_FRAMES):
-                proj = psum_proj.tile([P, BANK_FRAMES, W_ROWS], F32)
-                for f in range(BANK_FRAMES):
-                    joints = slice((first_frame + f) * V, (first_frame + f + 1) * V)
+            for a in range(SIDES):
+                for b in range(KT_PASSES):
+                    nc.scalar.copy(out=w_grouped_words[:, h, a, b], in_=w_flipped_rows[:, a, b])
+
+        def quantise_weights():
+            nc.vector.quantize_mx(
+                out=w_codes[:].rearrange("p h r -> p (h r)").bitcast(FP8X4),
+                scales=w_scales[:].rearrange("p h r -> p (h r)"),
+                in_=w_grouped[:],
+            )
+
+        groups = {}
+        xq = {}
+        banks = {}
+        moved = {}
+
+        def regroup(copy, k, h, first, last):
+            copy(
+                out=groups[k][h][:].rearrange("p (c j) -> p c j", j=PACK)[:, first:last].rearrange(
+                    "p (c i) j -> p c j i", i=4
+                ),
+                in_=raws[k][h][:, :, first:last].rearrange("p j (c i) -> p c j i", i=4),
+            )
+
+        def regroup_block(k):
+            groups[k] = []
+            for h in range(C_PASSES):
+                grouped = grouped_pool.tile([P, BLOCK * PACK], BF16, align_bytes=64)
+                groups[k].append(grouped)
+            if k == 0:
+                for first in range(0, BLOCK, FIRST_PIECE):
+                    regroup(nc.vector.tensor_copy, k, 0, first, first + FIRST_PIECE)
+                quantise_weights()
+            else:
+                regroup(nc.vector.tensor_copy, k, 0, 0, BLOCK)
+            regroup(nc.scalar.copy, k, 1, BLOCK - SCALAR_COLS, BLOCK)
+            regroup(nc.vector.tensor_copy, k, 1, 0, BLOCK - SCALAR_COLS)
+
+        def quantise_x(k, h):
+            if h == 0:
+                codes = xq_pool.tile([P, C_PASSES, BLOCK], U32, align_bytes=64)
+                scales = xq_pool.tile([P, C_PASSES, BLOCK], U8, align_bytes=64)
+                xq[k] = (codes, scales)
+            codes, scales = xq[k]
+            nc.vector.quantize_mx(
+                out=codes[:, h, :].bitcast(FP8X4), scales=scales[:, h, :], in_=groups[k][h][:]
+            )
+
+        def project(k):
+            codes, scales = xq[k]
+            banks[k] = []
+            for run in range(RUNS):
+                cols = slice(run * RUN, (run + 1) * RUN)
+                for a in range(SIDES):
+                    rows = slice(a * SIDE_ROWS, (a + 1) * SIDE_ROWS)
+                    bank = psum_proj.tile([P, RUN], F32, tag="bank")
                     for h in range(C_PASSES):
                         nc.tensor.matmul_mx(
-                            out=proj[:, f, :],
-                            lhsT=x_codes[:, h, joints].bitcast(FP8X4),
-                            lhsT_scale=x_scales[:, h, joints],
-                            rhs=w_codes[:, h, :].bitcast(FP8X4),
-                            rhs_scale=w_scales[:, h, :],
+                            out=bank[:],
+                            lhsT=w_codes[:, h, rows].bitcast(FP8X4),
+                            lhsT_scale=w_scales[:, h, rows],
+                            rhs=codes[:, h, cols].bitcast(FP8X4),
+                            rhs_scale=scales[:, h, cols],
                             start=(h == 0),
                             stop=(h == C_PASSES - 1),
                         )
-                t_word, u = divmod((g * GROUP_FRAMES + first_frame) // PAIR, PAIRS)
-                nc.scalar.copy(
-                    out=f_rows_view[:, t_word, u],
-                    in_=proj[:].rearrange("p e (i q) -> p i q e", q=OPERANDS),
+                    banks[k].append(bank)
+
+        def empty_and_move(k, copies):
+            n, part = divmod(k, BLOCKS)
+            if part == 0:
+                moved[n] = f_pool.tile(
+                    [P, KT_PASSES, OPERANDS * V * PACK], BF16, align_bytes=64, name="moved"
                 )
-
-        def quantise_pass(f_rows, g, codes, scales):
-            f_words = f_rows[:].bitcast(F32)
-            plane_words = INTER * FRAME_WORDS * OPERANDS
-            pass_words = P * OPERANDS
-            f_grouped = f_pool.tile([P, OPERANDS * V * PACK], BF16, align_bytes=64)
-            f_grouped_words = f_grouped[:].bitcast(F32).rearrange(
-                "p (o v u) -> p o v u", o=OPERANDS, v=V, u=2
-            )
-            for first_operand in range(0, OPERANDS, BANK_OPERANDS):
-                flipped = psum_flip.tile([P, BANK_OPERANDS, 2, V], F32, tag="flipped")
-                for o in range(BANK_OPERANDS):
-                    for u in range(2):
-                        first = u * plane_words + g * pass_words + first_operand + o
-                        nc.tensor.transpose(
-                            flipped[:, o, u, :],
-                            f_words[:, first : first + pass_words - OPERANDS + 1 : OPERANDS],
-                            ident[:],
-                        )
-                nc.scalar.copy(
-                    out=f_grouped_words[:, first_operand : first_operand + BANK_OPERANDS],
-                    in_=flipped[:].rearrange("p o u v -> p o v u"),
-                )
-            nc.vector.quantize_mx(out=codes.bitcast(FP8X4), scales=scales, in_=f_grouped[:])
-
-        def attend(n, f_rows):
-            f_codes = f_pool.tile([P, GROUPS, OPERANDS * V], U32, align_bytes=64)
-            f_scales = f_pool.tile([P, GROUPS, OPERANDS * V], U8, align_bytes=64)
-            for g in range(GROUPS):
-                quantise_pass(f_rows, g, f_codes[:, g, :], f_scales[:, g, :])
-
-            scores = psum_score.tile([P, S, V], F32)
-            for s in range(S):
-                fa_cols = slice(s * V, (s + 1) * V)
-                fb_cols = slice((S + s) * V, (S + s + 1) * V)
-                for g in range(GROUPS):
-                    nc.tensor.matmul_mx(
-                        out=scores[:, s, :],
-                        lhsT=f_codes[:, g, fb_cols].bitcast(FP8X4),
-                        lhsT_scale=f_scales[:, g, fb_cols],
-                        rhs=f_codes[:, g, fa_cols].bitcast(FP8X4),
-                        rhs_scale=f_scales[:, g, fa_cols],
-                        start=(g == 0),
-                        stop=(g == GROUPS - 1),
+            for run in range(RUNS):
+                rows = rows_pool.tile([P, SIDES, RUN], BF16)
+                for a in range(SIDES):
+                    copies[a](
+                        out=rows[:, a, :],
+                        in_=banks[k][run * SIDES + a][:].rearrange("p (j v) -> p v j", j=PACK),
                     )
+                t_word = part * RUNS + run
+                nc.sync.dma_start(
+                    out=moved[n][t_word:P:WORDS].rearrange("i b e -> i (b e)"),
+                    in_=rows[:].rearrange("p a e -> p (a e)"),
+                )
 
-            top = soft_pool.tile([P, S], F32)
-            nc.vector.tensor_reduce(out=top[:], in_=scores[:], axis=mybir.AxisListType.X, op=ALU.max)
-            shift = soft_pool.tile([P, S], F32)
+        fq = {}
+        soft = {}
+
+        def quantise_f(n, b, run):
+            if n not in fq:
+                codes = f_pool.tile([P, KT_PASSES, OPERANDS * V], U32, align_bytes=64, name="f_codes")
+                scales = f_pool.tile([P, KT_PASSES, OPERANDS * V], U8, align_bytes=64, name="f_scales")
+                fq[n] = (codes, scales)
+            codes, scales = fq[n]
+            cols = slice(run.start * SIDES * V, run.stop * SIDES * V)
+            nc.vector.quantize_mx(
+                out=codes[:, b, cols].bitcast(FP8X4),
+                scales=scales[:, b, cols],
+                in_=moved[n][:, b, cols.start * PACK : cols.stop * PACK],
+            )
+
+        def score(n, run, pool, tag):
+            codes, scales = fq[n]
+            scores = pool.tile([P, len(run), V], F32, name="scores", tag=tag)
+            for r, s in enumerate(run):
+                fa_cols = slice(SIDES * s * V, (SIDES * s + 1) * V)
+                fb_cols = slice((SIDES * s + 1) * V, (SIDES * s + 2) * V)
+                for b in range(KT_PASSES):
+                    nc.tensor.matmul_mx(
+                        out=scores[:, r, :],
+                        lhsT=codes[:, b, fb_cols].bitcast(FP8X4),
+                        lhsT_scale=scales[:, b, fb_cols],
+                        rhs=codes[:, b, fa_cols].bitcast(FP8X4),
+                        rhs_scale=scales[:, b, fa_cols],
+                        start=(b == 0),
+                        stop=(b == KT_PASSES - 1),
+                    )
+            soft[n, run.start] = {"scores": scores}
+
+        def find_top(n, run):
+            top = soft_pool.tile([P, len(run)], F32)
+            state = soft[n, run.start]
+            nc.vector.tensor_reduce(
+                out=top[:], in_=state["scores"][:], axis=mybir.AxisListType.X, op=ALU.max
+            )
+            shift = soft_pool.tile([P, len(run)], F32)
             nc.vector.tensor_scalar(
                 out=shift[:], in0=top[:], scalar1=-1.0 / KT, scalar2=None, op0=ALU.mult
             )
-            expd = soft_pool.tile([P, S, V], F32)
-            sums = soft_pool.tile([P, S], F32)
-            for s in range(S):
+            state["shift"] = shift
+
+        def exponentiate(n, run):
+            state = soft[n, run.start]
+            expd = soft_pool.tile([P, len(run), V], F32)
+            sums = soft_pool.tile([P, len(run)], F32)
+            for r in range(len(run)):
                 nc.scalar.activation(
-                    out=expd[:, s, :],
-                    in_=scores[:, s, :],
+                    out=expd[:, r, :],
+                    in_=state["scores"][:, r, :],
                     func=ACT.Exp,
-                    bias=shift[:, s : s + 1],
+                    bias=state["shift"][:, r : r + 1],
                     scale=1.0 / KT,
-                    accum_out=sums[:, s : s + 1],
+                    accum_out=sums[:, r : r + 1],
                 )
-            inverse = soft_pool.tile([P, S], F32)
-            nc.vector.reciprocal(out=inverse[:], in_=sums[:])
-            attn = soft_pool.tile([P, S, V], F32)
+            state["expd"], state["sums"] = expd, sums
+
+        def normalise(n, run):
+            state = soft[n, run.start]
+            inverse = soft_pool.tile([P, len(run)], F32)
+            nc.vector.reciprocal(out=inverse[:], in_=state["sums"][:])
+            attn = soft_pool.tile([P, len(run), V], F32)
             nc.vector.tensor_tensor(
                 out=attn[:],
-                in0=expd[:],
-                in1=inverse[:].unsqueeze(2).to_broadcast([P, S, V]),
+                in0=state["expd"][:],
+                in1=inverse[:].unsqueeze(2).to_broadcast([P, len(run), V]),
                 op=ALU.mult,
             )
+            state["attn"] = attn
 
-            attn_flipped = psum_score.tile([P, S, V], F32)
-            for s in range(S):
-                nc.tensor.transpose(attn_flipped[:, s, :], attn[:, s, :], ident[:])
-            result = soft_pool.tile([P, S, V], F32)
-            nc.vector.tensor_tensor(out=result[:], in0=attn_flipped[:], in1=adjacency[:], op=ALU.add)
-            nc.sync.dma_start(out=out[n].rearrange("s v w -> v s w"), in_=result[:])
+        def flip_back(n, run, pool, tag):
+            state = soft[n, run.start]
+            flipped = pool.tile([P, len(run), V], F32, name="flipped", tag=tag)
+            for r in range(len(run)):
+                nc.tensor.transpose(flipped[:, r, :], state["attn"][:, r, :], ident[:])
+            state["flipped"] = flipped
 
-        projected = {}
-        for n in range(N + SAMPLES_BEHIND):
-            if n < N:
-                f_rows = rows_pool.tile([P, T * W_ROWS], BF16)
-                for g in range(GROUPS):
-                    project_group(n, g, f_rows)
-                projected[n] = f_rows
-            if n >= SAMPLES_BEHIND:
-                attend(n - SAMPLES_BEHIND, projected[n - SAMPLES_BEHIND])
+        def add_and_store(n, run):
+            result = soft_pool.tile([P, len(run), V], F32)
+            nc.vector.tensor_tensor(
+                out=result[:],
+                in0=soft[n, run.start]["flipped"][:],
+                in1=adjacency[:, run.start : run.stop, :],
+                op=ALU.add,
+            )
+            nc.sync.dma_start(
+                out=out[n, run.start : run.stop].rearrange("s v w -> v s w"), in_=result[:]
+            )
+
+        every = range(S)
+        scalar_copies = [nc.scalar.copy, nc.scalar.copy]
+        both_copies = [nc.scalar.copy, nc.vector.tensor_copy]
+        for k in range(STEPS + 1):
+            n, phase = divmod(k - BLOCKS - 1, BLOCKS)
+            if k + AHEAD < STEPS:
+                load(k + AHEAD)
+            if n >= 0 and phase == 3:
+                flip_back(n, every, psum_score, "flipped")
+            if k < STEPS:
+                regroup_block(k)
+                quantise_x(k, 0)
+            if n >= 0 and phase == 0:
+                quantise_f(n, 0, every)
+            if n >= 0 and phase == 1:
+                quantise_f(n, 1, every)
+                score(n, every, psum_score, "scores")
+            if n >= 0 and phase == 2:
+                exponentiate(n, every)
+            if k > 0:
+                empty_and_move(k - 1, scalar_copies if k < STEPS else both_copies)
+            if k < STEPS:
+                quantise_x(k, 1)
+                project(k)
+            if n >= 0 and phase == 1:
+                find_top(n, every)
+            if n >= 0 and phase == 2:
+                normalise(n, every)
+            if n >= 0 and phase == 3:
+                add_and_store(n, every)
+
+        n = N - 1
+        halves = [range(0, S // 2), range(S // 2, S)]
+        for run in halves:
+            for b in range(KT_PASSES):
+                quantise_f(n, b, run)
+            score(n, run, psum_proj, "bank")
+        for run in halves:
+            find_top(n, run)
+            exponentiate(n, run)
+        for run in halves:
+            normalise(n, run)
+            flip_back(n, run, psum_proj, "bank")
+        for run in halves:
+            add_and_store(n, run)

@@ -181,6 +181,7 @@ def tile_unitagcn_pa_t_kernel(tc, x, A, PA, Wa, Wb, out):
                 moved[n] = f_pool.tile(
                     [P, KT_PASSES, OPERANDS * V * PACK], BF16, align_bytes=64, name="moved"
                 )
+            moves = []
             for run in range(RUNS):
                 rows = rows_pool.tile([P, SIDES, RUN], BF16)
                 for a in range(SIDES):
@@ -188,8 +189,9 @@ def tile_unitagcn_pa_t_kernel(tc, x, A, PA, Wa, Wb, out):
                         out=rows[:, a, :],
                         in_=banks[k][run * SIDES + a][:].rearrange("p (j v) -> p v j", j=PACK),
                     )
-                t_word = part * RUNS + run
-                nc.sync.dma_start(
+                moves.append((part * RUNS + run, rows))
+            for t_word, rows in moves:
+                nc.scalar.dma_start(
                     out=moved[n][t_word:P:WORDS].rearrange("i b e -> i (b e)"),
                     in_=rows[:].rearrange("p a e -> p (a e)"),
                 )

@@ -29,12 +29,14 @@ WORDS = T // PACK
 
 BLOCK = 1024
 BLOCKS = T * V // BLOCK
-RUN = PACK * V
-RUNS = BLOCK // RUN
+FRAMES = BLOCK // V
+PAIR = 2
 STEPS = N * BLOCKS
 AHEAD = 2
 FIRST_PIECE = BLOCK // 4
-SCALAR_COLS = 896
+SCALAR_COLS = 704
+FIRST_SCALAR_COLS = 512
+LAST_SCALAR_COLS = 1280
 
 FLOPS = 2 * SIDES * SIDE_ROWS * C * N * T * V + 2 * N * S * V * V * KT
 
@@ -44,12 +46,13 @@ def tile_unitagcn_pa_t_kernel(tc, x, A, PA, Wa, Wb, out):
     with ExitStack() as stack:
         consts = stack.enter_context(tc.tile_pool(name="consts", bufs=1))
         raw_pool = stack.enter_context(tc.tile_pool(name="raw", bufs=C_PASSES * (AHEAD + 1)))
-        grouped_pool = stack.enter_context(tc.tile_pool(name="grouped", bufs=4))
+        grouped_pool = stack.enter_context(tc.tile_pool(name="grouped", bufs=6))
         xq_pool = stack.enter_context(tc.tile_pool(name="xq", bufs=3))
-        rows_pool = stack.enter_context(tc.tile_pool(name="rows", bufs=4))
+        rows_pool = stack.enter_context(tc.tile_pool(name="rows", bufs=2))
         f_pool = stack.enter_context(tc.tile_pool(name="f", bufs=2))
         soft_pool = stack.enter_context(tc.tile_pool(name="soft", bufs=2))
-        psum_proj = stack.enter_context(tc.psum_pool(name="psum_proj", bufs=6))
+        psum_proj = stack.enter_context(tc.psum_pool(name="psum_proj", bufs=5))
+        psum_flip = stack.enter_context(tc.psum_pool(name="psum_flip", bufs=2))
         psum_score = stack.enter_context(tc.psum_pool(name="psum_score", bufs=1))
         stack.enter_context(tc.manual_schedule())
 
@@ -89,13 +92,12 @@ def tile_unitagcn_pa_t_kernel(tc, x, A, PA, Wa, Wb, out):
         w_words = w_rows[:].bitcast(F32).rearrange("p (a c) -> p a c", a=SIDES)
         w_grouped = consts.tile([P, C_PASSES * SIDES * SIDE_ROWS * PACK], BF16, align_bytes=64)
         w_grouped_words = w_grouped[:].bitcast(F32).rearrange(
-            "p (h a i b s u) -> p h a b i s u",
-            h=C_PASSES, a=SIDES, i=HALF, b=KT_PASSES, s=S, u=PAIRS,
+            "p (h i s a u) -> p h s i a u", h=C_PASSES, i=INTER, s=S, a=SIDES, u=PAIRS
         )
         w_codes = consts.tile([P, C_PASSES, SIDES * SIDE_ROWS], U32, align_bytes=64)
         w_scales = consts.tile([P, C_PASSES, SIDES * SIDE_ROWS], U8, align_bytes=64)
         for h in range(C_PASSES):
-            w_flipped = psum_proj.tile([P, SIDES, PAIRS, SIDE_ROWS], F32, tag="bank")
+            w_flipped = psum_flip.tile([P, SIDES, PAIRS, SIDE_ROWS], F32, tag="flip")
             for a in range(SIDES):
                 for u in range(PAIRS):
                     first = h * (K_PASS // 2) + u
@@ -104,12 +106,9 @@ def tile_unitagcn_pa_t_kernel(tc, x, A, PA, Wa, Wb, out):
                         w_words[:, a, first : first + K_PASS // 2 - 1 : PAIRS],
                         ident[:],
                     )
-            w_flipped_rows = w_flipped[:].rearrange(
-                "p a u (s b i) -> p a b i s u", s=S, b=KT_PASSES
-            )
-            for a in range(SIDES):
-                for b in range(KT_PASSES):
-                    nc.scalar.copy(out=w_grouped_words[:, h, a, b], in_=w_flipped_rows[:, a, b])
+            w_flipped_rows = w_flipped[:].rearrange("p a u (s i) -> p s i a u", s=S)
+            for s in range(S):
+                nc.scalar.copy(out=w_grouped_words[:, h, s], in_=w_flipped_rows[:, s])
 
         def quantise_weights():
             nc.vector.quantize_mx(
@@ -121,7 +120,7 @@ def tile_unitagcn_pa_t_kernel(tc, x, A, PA, Wa, Wb, out):
         groups = {}
         xq = {}
         banks = {}
-        moved = {}
+        f_rows = {}
 
         def regroup(copy, k, h, first, last):
             copy(
@@ -131,73 +130,104 @@ def tile_unitagcn_pa_t_kernel(tc, x, A, PA, Wa, Wb, out):
                 in_=raws[k][h][:, :, first:last].rearrange("p j (c i) -> p c j i", i=4),
             )
 
-        def regroup_block(k):
+        def vector_cols(k, h):
+            if k == 0:
+                share = FIRST_SCALAR_COLS
+            else:
+                share = LAST_SCALAR_COLS if k == STEPS - 1 else SCALAR_COLS
+            return BLOCK - (min(share, BLOCK) if h == 1 else max(share - BLOCK, 0))
+
+        def regroup_on_scalar(k):
             groups[k] = []
             for h in range(C_PASSES):
                 grouped = grouped_pool.tile([P, BLOCK * PACK], BF16, align_bytes=64)
                 groups[k].append(grouped)
-            if k == 0:
-                for first in range(0, BLOCK, FIRST_PIECE):
-                    regroup(nc.vector.tensor_copy, k, 0, first, first + FIRST_PIECE)
-                quantise_weights()
-            else:
-                regroup(nc.vector.tensor_copy, k, 0, 0, BLOCK)
-            regroup(nc.scalar.copy, k, 1, BLOCK - SCALAR_COLS, BLOCK)
-            regroup(nc.vector.tensor_copy, k, 1, 0, BLOCK - SCALAR_COLS)
+            for h in range(C_PASSES):
+                if vector_cols(k, h) < BLOCK:
+                    regroup(nc.scalar.copy, k, h, vector_cols(k, h), BLOCK)
 
-        def quantise_x(k, h):
-            if h == 0:
+        def regroup_on_vector(k):
+            for h in range(C_PASSES):
+                width = FIRST_PIECE if (k, h) == (0, 0) else vector_cols(k, h)
+                for first in range(0, vector_cols(k, h), max(width, 1)):
+                    regroup(nc.vector.tensor_copy, k, h, first, first + width)
+                if (k, h) == (0, 0):
+                    quantise_weights()
+
+        def quantise_x(k, h, first=0, last=BLOCK):
+            if k not in xq:
                 codes = xq_pool.tile([P, C_PASSES, BLOCK], U32, align_bytes=64)
                 scales = xq_pool.tile([P, C_PASSES, BLOCK], U8, align_bytes=64)
                 xq[k] = (codes, scales)
             codes, scales = xq[k]
             nc.vector.quantize_mx(
-                out=codes[:, h, :].bitcast(FP8X4), scales=scales[:, h, :], in_=groups[k][h][:]
+                out=codes[:, h, first:last].bitcast(FP8X4),
+                scales=scales[:, h, first:last],
+                in_=groups[k][h][:, first * PACK : last * PACK],
             )
 
-        def project(k):
+        def project(k, pairs_of_frames=range(FRAMES // PAIR)):
             codes, scales = xq[k]
-            banks[k] = []
-            for run in range(RUNS):
-                cols = slice(run * RUN, (run + 1) * RUN)
-                for a in range(SIDES):
-                    rows = slice(a * SIDE_ROWS, (a + 1) * SIDE_ROWS)
-                    bank = psum_proj.tile([P, RUN], F32, tag="bank")
+            for pair in pairs_of_frames:
+                bank = psum_proj.tile([P, PAIR, SIDES * SIDE_ROWS], F32, tag="bank")
+                for e in range(PAIR):
+                    frame = pair * PAIR + e
+                    joints = slice(frame * V, (frame + 1) * V)
                     for h in range(C_PASSES):
                         nc.tensor.matmul_mx(
-                            out=bank[:],
-                            lhsT=w_codes[:, h, rows].bitcast(FP8X4),
-                            lhsT_scale=w_scales[:, h, rows],
-                            rhs=codes[:, h, cols].bitcast(FP8X4),
-                            rhs_scale=scales[:, h, cols],
+                            out=bank[:, e, :],
+                            lhsT=codes[:, h, joints].bitcast(FP8X4),
+                            lhsT_scale=scales[:, h, joints],
+                            rhs=w_codes[:, h, :].bitcast(FP8X4),
+                            rhs_scale=w_scales[:, h, :],
                             start=(h == 0),
                             stop=(h == C_PASSES - 1),
                         )
-                    banks[k].append(bank)
+                banks[k, pair] = bank
 
-        def empty_and_move(k, copies):
+        def empty_banks(k, copies, pairs_of_frames=range(FRAMES // PAIR)):
             n, part = divmod(k, BLOCKS)
-            if part == 0:
-                moved[n] = f_pool.tile(
-                    [P, KT_PASSES, OPERANDS * V * PACK], BF16, align_bytes=64, name="moved"
-                )
-            moves = []
-            for run in range(RUNS):
-                rows = rows_pool.tile([P, SIDES, RUN], BF16)
-                for a in range(SIDES):
-                    copies[a](
-                        out=rows[:, a, :],
-                        in_=banks[k][run * SIDES + a][:].rearrange("p (j v) -> p v j", j=PACK),
-                    )
-                moves.append((part * RUNS + run, rows))
-            for t_word, rows in moves:
-                nc.scalar.dma_start(
-                    out=moved[n][t_word:P:WORDS].rearrange("i b e -> i (b e)"),
-                    in_=rows[:].rearrange("p a e -> p (a e)"),
+            if n not in f_rows:
+                f_rows[n] = rows_pool.tile([P, T * SIDES * SIDE_ROWS], BF16, name="f_rows")
+            view = f_rows[n][:].rearrange(
+                "p (u i t q e) -> p t u i q e", u=PAIRS, i=INTER, t=WORDS, q=OPERANDS, e=PAIR
+            )
+            for pair in pairs_of_frames:
+                t_word, u = divmod(part * (FRAMES // PAIR) + pair, PAIRS)
+                copies[pair % len(copies)](
+                    out=view[:, t_word, u],
+                    in_=banks[k, pair][:].rearrange("p e (i q) -> p i q e", q=OPERANDS),
                 )
 
+        flips = {}
+        turned = {}
         fq = {}
         soft = {}
+
+        def flip(n, b, s, pool, tag):
+            words = f_rows[n][:].bitcast(F32)
+            bank = pool.tile([P, SIDES, PAIRS, V], F32, tag=tag)
+            for a in range(SIDES):
+                for u in range(PAIRS):
+                    first = (u * KT_PASSES + b) * P * OPERANDS + SIDES * s + a
+                    nc.tensor.transpose(
+                        bank[:, a, u, :],
+                        words[:, first : first + (P - 1) * OPERANDS + 1 : OPERANDS],
+                        ident[:],
+                    )
+            flips[n, b, s] = bank
+
+        def empty_flip(copy, n, b, s):
+            if (n, b) not in turned:
+                turned[n, b] = f_pool.tile(
+                    [P, OPERANDS * V * PACK], BF16, align_bytes=64, name="turned"
+                )
+            copy(
+                out=turned[n, b][:].bitcast(F32).rearrange(
+                    "p (s a v u) -> p s a v u", s=S, a=SIDES, v=V, u=PAIRS
+                )[:, s],
+                in_=flips[n, b, s][:].rearrange("p a u v -> p a v u"),
+            )
 
         def quantise_f(n, b, run):
             if n not in fq:
@@ -209,7 +239,7 @@ def tile_unitagcn_pa_t_kernel(tc, x, A, PA, Wa, Wb, out):
             nc.vector.quantize_mx(
                 out=codes[:, b, cols].bitcast(FP8X4),
                 scales=scales[:, b, cols],
-                in_=moved[n][:, b, cols.start * PACK : cols.stop * PACK],
+                in_=turned[n, b][:, cols.start * PACK : cols.stop * PACK],
             )
 
         def score(n, run, pool, tag):
@@ -289,48 +319,87 @@ def tile_unitagcn_pa_t_kernel(tc, x, A, PA, Wa, Wb, out):
                 out=out[n, run.start : run.stop].rearrange("s v w -> v s w"), in_=result[:]
             )
 
+        pairs = [range(0, S // 2), range(S // 2, S)]
         every = range(S)
-        scalar_copies = [nc.scalar.copy, nc.scalar.copy]
-        both_copies = [nc.scalar.copy, nc.vector.tensor_copy]
-        for k in range(STEPS + 1):
-            n, phase = divmod(k - BLOCKS - 1, BLOCKS)
+
+        def flip_part(n, part, copies, pool, tag):
+            b, half = divmod(part, 2)
+            for s in pairs[half]:
+                flip(n, b, s, pool, tag)
+                empty_flip(copies[s % len(copies)], n, b, s)
+
+        def quantise_part(n, part):
+            b, half = divmod(part, 2)
+            quantise_f(n, b, pairs[half])
+
+        regroup_on_scalar(0)
+        for k in range(STEPS):
             if k + AHEAD < STEPS:
                 load(k + AHEAD)
-            if n >= 0 and phase == 3:
-                flip_back(n, every, psum_score, "flipped")
-            if k < STEPS:
-                regroup_block(k)
+            phases = {k - BLOCKS * (n + 1) - 1: n for n in range(N)}
+            if 6 in phases:
+                flip_back(phases[6], every, psum_score, "score")
+            regroup_on_vector(k)
+            if k + 1 < STEPS:
+                regroup_on_scalar(k + 1)
+            if 5 in phases:
+                exponentiate(phases[5], every)
+            if k < STEPS - 1:
                 quantise_x(k, 0)
-            if n >= 0 and phase == 0:
-                quantise_f(n, 0, every)
-            if n >= 0 and phase == 1:
-                quantise_f(n, 1, every)
-                score(n, every, psum_score, "scores")
-            if n >= 0 and phase == 2:
-                exponentiate(n, every)
+            for part in range(4):
+                if part + 1 in phases:
+                    quantise_part(phases[part + 1], part)
+            if 4 in phases:
+                score(phases[4], every, psum_score, "score")
             if k > 0:
-                empty_and_move(k - 1, scalar_copies if k < STEPS else both_copies)
-            if k < STEPS:
+                empty_banks(k - 1, [nc.scalar.copy])
+            for part in range(4):
+                if part in phases:
+                    flip_part(phases[part], part, [nc.scalar.copy], psum_flip, "flip")
+            if k < STEPS - 1:
                 quantise_x(k, 1)
                 project(k)
-            if n >= 0 and phase == 1:
-                find_top(n, every)
-            if n >= 0 and phase == 2:
-                normalise(n, every)
-            if n >= 0 and phase == 3:
-                add_and_store(n, every)
+            if 4 in phases:
+                find_top(phases[4], every)
+            if 5 in phases:
+                normalise(phases[5], every)
+            if 6 in phases:
+                add_and_store(phases[6], every)
 
-        n = N - 1
-        halves = [range(0, S // 2), range(S // 2, S)]
-        for run in halves:
-            for b in range(KT_PASSES):
-                quantise_f(n, b, run)
-            score(n, run, psum_proj, "bank")
-        for run in halves:
-            find_top(n, run)
-            exponentiate(n, run)
-        for run in halves:
-            normalise(n, run)
-            flip_back(n, run, psum_proj, "bank")
-        for run in halves:
-            add_and_store(n, run)
+        before, last = N - 2, N - 1
+        both = [nc.scalar.copy, nc.vector.tensor_copy]
+        flip_part(before, 3, [nc.scalar.copy], psum_flip, "flip")
+        half_pairs = FRAMES // PAIR // 2
+        for half in range(2):
+            for h in range(C_PASSES):
+                quantise_x(STEPS - 1, h, half * BLOCK // 2, (half + 1) * BLOCK // 2)
+            project(STEPS - 1, range(half * half_pairs, (half + 1) * half_pairs))
+        quantise_part(before, 2)
+        quantise_part(before, 3)
+        empty_banks(STEPS - 1, both)
+        score(before, every, psum_score, "score")
+        flip_part(last, 0, both, psum_proj, "bank")
+        flip_part(last, 2, both, psum_proj, "bank")
+        find_top(before, every)
+        quantise_part(last, 0)
+        quantise_part(last, 2)
+        flip_part(last, 1, both, psum_proj, "bank")
+        flip_part(last, 3, both, psum_proj, "bank")
+        exponentiate(before, every)
+        score(last, pairs[0], psum_flip, "flip")
+        quantise_part(last, 1)
+        quantise_part(last, 3)
+        find_top(last, pairs[0])
+        score(last, pairs[1], psum_flip, "flip")
+        exponentiate(last, pairs[0])
+        normalise(before, every)
+        flip_back(before, every, psum_score, "score")
+        find_top(last, pairs[1])
+        normalise(last, pairs[0])
+        exponentiate(last, pairs[1])
+        flip_back(last, pairs[0], psum_proj, "bank")
+        add_and_store(before, every)
+        add_and_store(last, pairs[0])
+        normalise(last, pairs[1])
+        flip_back(last, pairs[1], psum_proj, "bank")
+        add_and_store(last, pairs[1])

@@ -20,7 +20,6 @@ PAIRS = PACK // 2
 K_PASS = P * PACK
 C_PASSES = C // K_PASS
 KT_PASSES = KT // K_PASS
-HALF = INTER // KT_PASSES
 
 SIDES = 2
 SIDE_ROWS = S * INTER
@@ -31,12 +30,12 @@ BLOCK = 1024
 BLOCKS = T * V // BLOCK
 FRAMES = BLOCK // V
 PAIR = 2
+BANKS = FRAMES // PAIR
 STEPS = N * BLOCKS
 AHEAD = 2
-FIRST_PIECE = BLOCK // 4
+PIECE = BLOCK // 4
 SCALAR_COLS = 704
-FIRST_SCALAR_COLS = 512
-LAST_SCALAR_COLS = 1280
+LAST_SCALAR_COLS = 896
 
 FLOPS = 2 * SIDES * SIDE_ROWS * C * N * T * V + 2 * N * S * V * V * KT
 
@@ -46,39 +45,51 @@ def tile_unitagcn_pa_t_kernel(tc, x, A, PA, Wa, Wb, out):
     with ExitStack() as stack:
         consts = stack.enter_context(tc.tile_pool(name="consts", bufs=1))
         raw_pool = stack.enter_context(tc.tile_pool(name="raw", bufs=C_PASSES * (AHEAD + 1)))
-        grouped_pool = stack.enter_context(tc.tile_pool(name="grouped", bufs=6))
+        grouped_pool = stack.enter_context(tc.tile_pool(name="grouped", bufs=C_PASSES * 3))
         xq_pool = stack.enter_context(tc.tile_pool(name="xq", bufs=3))
         rows_pool = stack.enter_context(tc.tile_pool(name="rows", bufs=2))
         f_pool = stack.enter_context(tc.tile_pool(name="f", bufs=2))
-        soft_pool = stack.enter_context(tc.tile_pool(name="soft", bufs=2))
+        soft_pool = stack.enter_context(tc.tile_pool(name="soft", bufs=3))
         psum_proj = stack.enter_context(tc.psum_pool(name="psum_proj", bufs=5))
         psum_flip = stack.enter_context(tc.psum_pool(name="psum_flip", bufs=2))
         psum_score = stack.enter_context(tc.psum_pool(name="psum_score", bufs=1))
         stack.enter_context(tc.manual_schedule())
 
         raws = {}
+        groups = {}
 
-        def load(k, pieces=1):
+        def allocate(k):
+            raws[k] = [
+                raw_pool.tile([P, PACK, BLOCK], BF16, name="raw") for h in range(C_PASSES)
+            ]
+            groups[k] = [
+                grouped_pool.tile([P, BLOCK * PACK], BF16, align_bytes=64, name="grouped")
+                for h in range(C_PASSES)
+            ]
+
+        def load(k, h, first=0, last=BLOCK):
             n, part = divmod(k, BLOCKS)
             x_rows = x[n].rearrange("(h p j) t v -> h p j (t v)", h=C_PASSES, p=P, j=PACK)
-            raws[k] = []
+            nc.sync.dma_start(
+                out=raws[k][h][:, :, first:last],
+                in_=x_rows[h][:, :, part * BLOCK + first : part * BLOCK + last],
+            )
+
+        def load_block(k):
+            allocate(k)
             for h in range(C_PASSES):
-                raw = raw_pool.tile([P, PACK, BLOCK], BF16)
-                width = BLOCK // pieces
-                for first in range(0, BLOCK, width):
-                    column = part * BLOCK + first
-                    nc.sync.dma_start(
-                        out=raw[:, :, first : first + width],
-                        in_=x_rows[h][:, :, column : column + width],
-                    )
-                raws[k].append(raw)
+                load(k, h)
 
         w_rows = consts.tile([P, SIDES * C], BF16)
         nc.scalar.dma_start(out=w_rows[:, 0:C], in_=Wa.rearrange("s i c -> (s i) c"))
         nc.scalar.dma_start(out=w_rows[:, C : 2 * C], in_=Wb.rearrange("s i c -> (s i) c"))
-        load(0, pieces=BLOCK // FIRST_PIECE)
+        allocate(0)
+        for half in range(2):
+            for h in range(C_PASSES):
+                for piece in range(2 * half, 2 * half + 2):
+                    load(0, h, piece * PIECE, (piece + 1) * PIECE)
         for k in range(1, AHEAD):
-            load(k)
+            load_block(k)
         a_rows = consts.tile([P, S, V], BF16)
         pa_rows = consts.tile([P, S, V], BF16)
         nc.scalar.dma_start(out=a_rows[:], in_=A.rearrange("s v w -> v s w"))
@@ -96,19 +107,21 @@ def tile_unitagcn_pa_t_kernel(tc, x, A, PA, Wa, Wb, out):
         )
         w_codes = consts.tile([P, C_PASSES, SIDES * SIDE_ROWS], U32, align_bytes=64)
         w_scales = consts.tile([P, C_PASSES, SIDES * SIDE_ROWS], U8, align_bytes=64)
-        for h in range(C_PASSES):
-            w_flipped = psum_flip.tile([P, SIDES, PAIRS, SIDE_ROWS], F32, tag="flip")
-            for a in range(SIDES):
-                for u in range(PAIRS):
-                    first = h * (K_PASS // 2) + u
-                    nc.tensor.transpose(
-                        w_flipped[:, a, u, :],
-                        w_words[:, a, first : first + K_PASS // 2 - 1 : PAIRS],
-                        ident[:],
-                    )
-            w_flipped_rows = w_flipped[:].rearrange("p a u (s i) -> p s i a u", s=S)
-            for s in range(S):
-                nc.scalar.copy(out=w_grouped_words[:, h, s], in_=w_flipped_rows[:, s])
+
+        def regroup_weights():
+            for h in range(C_PASSES):
+                bank = psum_flip.tile([P, SIDES, PAIRS, SIDE_ROWS], F32, tag="flip")
+                for a in range(SIDES):
+                    for u in range(PAIRS):
+                        first = h * (K_PASS // 2) + u
+                        nc.tensor.transpose(
+                            bank[:, a, u, :],
+                            w_words[:, a, first : first + K_PASS // 2 - 1 : PAIRS],
+                            ident[:],
+                        )
+                rows = bank[:].rearrange("p a u (s i) -> p s i a u", s=S)
+                for s in range(S):
+                    nc.scalar.copy(out=w_grouped_words[:, h, s], in_=rows[:, s])
 
         def quantise_weights():
             nc.vector.quantize_mx(
@@ -117,7 +130,6 @@ def tile_unitagcn_pa_t_kernel(tc, x, A, PA, Wa, Wb, out):
                 in_=w_grouped[:],
             )
 
-        groups = {}
         xq = {}
         banks = {}
         f_rows = {}
@@ -131,28 +143,18 @@ def tile_unitagcn_pa_t_kernel(tc, x, A, PA, Wa, Wb, out):
             )
 
         def vector_cols(k, h):
-            if k == 0:
-                share = FIRST_SCALAR_COLS
-            else:
-                share = LAST_SCALAR_COLS if k == STEPS - 1 else SCALAR_COLS
+            share = LAST_SCALAR_COLS if k == STEPS - 1 else SCALAR_COLS
             return BLOCK - (min(share, BLOCK) if h == 1 else max(share - BLOCK, 0))
 
         def regroup_on_scalar(k):
-            groups[k] = []
-            for h in range(C_PASSES):
-                grouped = grouped_pool.tile([P, BLOCK * PACK], BF16, align_bytes=64)
-                groups[k].append(grouped)
             for h in range(C_PASSES):
                 if vector_cols(k, h) < BLOCK:
                     regroup(nc.scalar.copy, k, h, vector_cols(k, h), BLOCK)
 
         def regroup_on_vector(k):
             for h in range(C_PASSES):
-                width = FIRST_PIECE if (k, h) == (0, 0) else vector_cols(k, h)
-                for first in range(0, vector_cols(k, h), max(width, 1)):
-                    regroup(nc.vector.tensor_copy, k, h, first, first + width)
-                if (k, h) == (0, 0):
-                    quantise_weights()
+                if vector_cols(k, h) > 0:
+                    regroup(nc.vector.tensor_copy, k, h, 0, vector_cols(k, h))
 
         def quantise_x(k, h, first=0, last=BLOCK):
             if k not in xq:
@@ -166,9 +168,16 @@ def tile_unitagcn_pa_t_kernel(tc, x, A, PA, Wa, Wb, out):
                 in_=groups[k][h][:, first * PACK : last * PACK],
             )
 
-        def project(k, pairs_of_frames=range(FRAMES // PAIR)):
+        def quantise_half(k, half):
+            for h in range(C_PASSES):
+                quantise_x(k, h, half * BLOCK // 2, (half + 1) * BLOCK // 2)
+
+        all_banks = range(BANKS)
+        half_banks = [range(0, BANKS // 2), range(BANKS // 2, BANKS)]
+
+        def project(k, some_banks):
             codes, scales = xq[k]
-            for pair in pairs_of_frames:
+            for pair in some_banks:
                 bank = psum_proj.tile([P, PAIR, SIDES * SIDE_ROWS], F32, tag="bank")
                 for e in range(PAIR):
                     frame = pair * PAIR + e
@@ -185,15 +194,15 @@ def tile_unitagcn_pa_t_kernel(tc, x, A, PA, Wa, Wb, out):
                         )
                 banks[k, pair] = bank
 
-        def empty_banks(k, copies, pairs_of_frames=range(FRAMES // PAIR)):
+        def empty_banks(k, some_banks, copies):
             n, part = divmod(k, BLOCKS)
             if n not in f_rows:
                 f_rows[n] = rows_pool.tile([P, T * SIDES * SIDE_ROWS], BF16, name="f_rows")
             view = f_rows[n][:].rearrange(
                 "p (u i t q e) -> p t u i q e", u=PAIRS, i=INTER, t=WORDS, q=OPERANDS, e=PAIR
             )
-            for pair in pairs_of_frames:
-                t_word, u = divmod(part * (FRAMES // PAIR) + pair, PAIRS)
+            for pair in some_banks:
+                t_word, u = divmod(part * BANKS + pair, PAIRS)
                 copies[pair % len(copies)](
                     out=view[:, t_word, u],
                     in_=banks[k, pair][:].rearrange("p e (i q) -> p i q e", q=OPERANDS),
@@ -203,39 +212,46 @@ def tile_unitagcn_pa_t_kernel(tc, x, A, PA, Wa, Wb, out):
         turned = {}
         fq = {}
         soft = {}
+        every = range(S)
+        halves = [range(0, S // 2), range(S // 2, S)]
 
-        def flip(n, b, s, pool, tag):
+        def flip(n, part, pool, tag):
+            b, half = divmod(part, 2)
             words = f_rows[n][:].bitcast(F32)
-            bank = pool.tile([P, SIDES, PAIRS, V], F32, tag=tag)
-            for a in range(SIDES):
-                for u in range(PAIRS):
-                    first = (u * KT_PASSES + b) * P * OPERANDS + SIDES * s + a
-                    nc.tensor.transpose(
-                        bank[:, a, u, :],
-                        words[:, first : first + (P - 1) * OPERANDS + 1 : OPERANDS],
-                        ident[:],
-                    )
-            flips[n, b, s] = bank
+            for s in halves[half]:
+                bank = pool.tile([P, SIDES, PAIRS, V], F32, tag=tag)
+                for a in range(SIDES):
+                    for u in range(PAIRS):
+                        first = (u * KT_PASSES + b) * P * OPERANDS + SIDES * s + a
+                        nc.tensor.transpose(
+                            bank[:, a, u, :],
+                            words[:, first : first + (P - 1) * OPERANDS + 1 : OPERANDS],
+                            ident[:],
+                        )
+                flips[n, b, s] = bank
 
-        def empty_flip(copy, n, b, s):
+        def empty_flips(n, part, copies):
+            b, half = divmod(part, 2)
             if (n, b) not in turned:
                 turned[n, b] = f_pool.tile(
                     [P, OPERANDS * V * PACK], BF16, align_bytes=64, name="turned"
                 )
-            copy(
-                out=turned[n, b][:].bitcast(F32).rearrange(
-                    "p (s a v u) -> p s a v u", s=S, a=SIDES, v=V, u=PAIRS
-                )[:, s],
-                in_=flips[n, b, s][:].rearrange("p a u v -> p a v u"),
+            view = turned[n, b][:].bitcast(F32).rearrange(
+                "p (s a v u) -> p s a v u", s=S, a=SIDES, v=V, u=PAIRS
             )
+            for s in halves[half]:
+                copies[s % len(copies)](
+                    out=view[:, s], in_=flips[n, b, s][:].rearrange("p a u v -> p a v u")
+                )
 
-        def quantise_f(n, b, run):
+        def quantise_f(n, part):
             if n not in fq:
                 codes = f_pool.tile([P, KT_PASSES, OPERANDS * V], U32, align_bytes=64, name="f_codes")
                 scales = f_pool.tile([P, KT_PASSES, OPERANDS * V], U8, align_bytes=64, name="f_scales")
                 fq[n] = (codes, scales)
             codes, scales = fq[n]
-            cols = slice(run.start * SIDES * V, run.stop * SIDES * V)
+            b, half = divmod(part, 2)
+            cols = slice(halves[half].start * SIDES * V, halves[half].stop * SIDES * V)
             nc.vector.quantize_mx(
                 out=codes[:, b, cols].bitcast(FP8X4),
                 scales=scales[:, b, cols],
@@ -319,87 +335,109 @@ def tile_unitagcn_pa_t_kernel(tc, x, A, PA, Wa, Wb, out):
                 out=out[n, run.start : run.stop].rearrange("s v w -> v s w"), in_=result[:]
             )
 
-        pairs = [range(0, S // 2), range(S // 2, S)]
-        every = range(S)
+        only_scalar = [nc.scalar.copy]
+        parts = range(2 * KT_PASSES)
 
-        def flip_part(n, part, copies, pool, tag):
-            b, half = divmod(part, 2)
-            for s in pairs[half]:
-                flip(n, b, s, pool, tag)
-                empty_flip(copies[s % len(copies)], n, b, s)
+        def first(n):
+            return BLOCKS * (n + 1) + 1
 
-        def quantise_part(n, part):
-            b, half = divmod(part, 2)
-            quantise_f(n, b, pairs[half])
+        def flipped(n, part):
+            return first(n) + (min(part, 2) if n == N - 2 else part)
 
-        regroup_on_scalar(0)
-        for k in range(STEPS):
+        def scored(n):
+            return first(n) + len(parts)
+
+        load_block(AHEAD)
+        for half in range(2):
+            left, middle, right = (column + half * BLOCK // 2 for column in (0, PIECE, 2 * PIECE))
+            regroup(nc.scalar.copy, 0, 1, left, middle)
+            for piece in (left, middle):
+                regroup(nc.vector.tensor_copy, 0, 0, piece, piece + PIECE)
+            regroup(nc.vector.tensor_copy, 0, 1, middle, right)
+            if half == 0:
+                regroup_weights()
+            quantise_half(0, half)
+            if half == 0:
+                quantise_weights()
+            project(0, half_banks[half])
+        empty_banks(0, half_banks[0], only_scalar)
+        regroup_on_scalar(1)
+        empty_banks(0, half_banks[1], only_scalar)
+
+        for k in range(1, STEPS):
             if k + AHEAD < STEPS:
-                load(k + AHEAD)
-            phases = {k - BLOCKS * (n + 1) - 1: n for n in range(N)}
-            if 6 in phases:
-                flip_back(phases[6], every, psum_score, "score")
+                load_block(k + AHEAD)
+            for n in range(N - 1):
+                if k == scored(n) + 2:
+                    flip_back(n, every, psum_score, "score")
             regroup_on_vector(k)
             if k + 1 < STEPS:
                 regroup_on_scalar(k + 1)
-            if 5 in phases:
-                exponentiate(phases[5], every)
+            for n in range(N - 1):
+                if k == scored(n) + 1:
+                    exponentiate(n, every)
             if k < STEPS - 1:
                 quantise_x(k, 0)
-            for part in range(4):
-                if part + 1 in phases:
-                    quantise_part(phases[part + 1], part)
-            if 4 in phases:
-                score(phases[4], every, psum_score, "score")
-            if k > 0:
-                empty_banks(k - 1, [nc.scalar.copy])
-            for part in range(4):
-                if part in phases:
-                    flip_part(phases[part], part, [nc.scalar.copy], psum_flip, "flip")
+            for n in range(N - 1):
+                for part in parts:
+                    if k == flipped(n, part) + 1:
+                        quantise_f(n, part)
+                if k == scored(n):
+                    score(n, every, psum_score, "score")
+            due = [(n, part) for n in range(N - 1) for part in parts if k == flipped(n, part)]
+            for n, part in due[1:]:
+                flip(n, part, psum_flip, "flip")
+                empty_flips(n, part, only_scalar)
+            if k > 1:
+                empty_banks(k - 1, all_banks, only_scalar)
+            for n, part in due[:1]:
+                flip(n, part, psum_flip, "flip")
+                empty_flips(n, part, only_scalar)
             if k < STEPS - 1:
                 quantise_x(k, 1)
-                project(k)
-            if 4 in phases:
-                find_top(phases[4], every)
-            if 5 in phases:
-                normalise(phases[5], every)
-            if 6 in phases:
-                add_and_store(phases[6], every)
+                project(k, all_banks)
+                for n in range(N - 1):
+                    if k == scored(n):
+                        find_top(n, every)
+            for n in range(N - 1):
+                if k == scored(n) + 1:
+                    normalise(n, every)
+                if k == scored(n) + 2:
+                    add_and_store(n, every)
 
         before, last = N - 2, N - 1
-        both = [nc.scalar.copy, nc.vector.tensor_copy]
-        flip_part(before, 3, [nc.scalar.copy], psum_flip, "flip")
-        half_pairs = FRAMES // PAIR // 2
         for half in range(2):
-            for h in range(C_PASSES):
-                quantise_x(STEPS - 1, h, half * BLOCK // 2, (half + 1) * BLOCK // 2)
-            project(STEPS - 1, range(half * half_pairs, (half + 1) * half_pairs))
-        quantise_part(before, 2)
-        quantise_part(before, 3)
-        empty_banks(STEPS - 1, both)
+            quantise_half(STEPS - 1, half)
+            project(STEPS - 1, half_banks[half])
+        empty_banks(STEPS - 1, half_banks[0], [nc.vector.tensor_copy])
+        empty_banks(STEPS - 1, half_banks[1], only_scalar)
+        for part in parts[2:]:
+            quantise_f(before, part)
         score(before, every, psum_score, "score")
-        flip_part(last, 0, both, psum_proj, "bank")
-        flip_part(last, 2, both, psum_proj, "bank")
         find_top(before, every)
-        quantise_part(last, 0)
-        quantise_part(last, 2)
-        flip_part(last, 1, both, psum_proj, "bank")
-        flip_part(last, 3, both, psum_proj, "bank")
+        for part in (0, 2):
+            flip(last, part, psum_proj, "bank")
+            empty_flips(last, part, only_scalar)
         exponentiate(before, every)
-        score(last, pairs[0], psum_flip, "flip")
-        quantise_part(last, 1)
-        quantise_part(last, 3)
-        find_top(last, pairs[0])
-        score(last, pairs[1], psum_flip, "flip")
-        exponentiate(last, pairs[0])
+        for part in (0, 2):
+            quantise_f(last, part)
+        for part in (1, 3):
+            flip(last, part, psum_proj, "bank")
+            empty_flips(last, part, only_scalar)
+        score(last, halves[0], psum_flip, "flip")
         normalise(before, every)
+        find_top(last, halves[0])
+        exponentiate(last, halves[0])
+        for part in (1, 3):
+            quantise_f(last, part)
+        score(last, halves[1], psum_flip, "flip")
         flip_back(before, every, psum_score, "score")
-        find_top(last, pairs[1])
-        normalise(last, pairs[0])
-        exponentiate(last, pairs[1])
-        flip_back(last, pairs[0], psum_proj, "bank")
+        normalise(last, halves[0])
+        find_top(last, halves[1])
+        exponentiate(last, halves[1])
+        flip_back(last, halves[0], psum_proj, "bank")
         add_and_store(before, every)
-        add_and_store(last, pairs[0])
-        normalise(last, pairs[1])
-        flip_back(last, pairs[1], psum_proj, "bank")
-        add_and_store(last, pairs[1])
+        normalise(last, halves[1])
+        add_and_store(last, halves[0])
+        flip_back(last, halves[1], psum_proj, "bank")
+        add_and_store(last, halves[1])

@@ -34,8 +34,8 @@ BANKS = FRAMES // PAIR
 STEPS = N * BLOCKS
 AHEAD = 2
 PIECE = BLOCK // 4
-SCALAR_COLS = 704
-LAST_SCALAR_COLS = 896
+SCALAR_COLS = 576
+LAST_SCALAR_COLS = 768
 
 FLOPS = 2 * SIDES * SIDE_ROWS * C * N * T * V + 2 * N * S * V * V * KT
 

@@ -34,8 +34,10 @@ BANKS = FRAMES // PAIR
 STEPS = N * BLOCKS
 AHEAD = 2
 PIECE = BLOCK // 4
-SCALAR_COLS = 576
-LAST_SCALAR_COLS = 768
+SCALAR_COLS = 704
+LAST_SCALAR_COLS = 896
+MIX_COLS = 256
+MIX_RUN = 128
 
 FLOPS = 2 * SIDES * SIDE_ROWS * C * N * T * V + 2 * N * S * V * V * KT
 
@@ -50,7 +52,8 @@ def tile_unitagcn_pa_t_kernel(tc, x, A, PA, Wa, Wb, out):
         rows_pool = stack.enter_context(tc.tile_pool(name="rows", bufs=2))
         f_pool = stack.enter_context(tc.tile_pool(name="f", bufs=2))
         soft_pool = stack.enter_context(tc.tile_pool(name="soft", bufs=3))
-        psum_proj = stack.enter_context(tc.psum_pool(name="psum_proj", bufs=5))
+        psum_proj = stack.enter_context(tc.psum_pool(name="psum_proj", bufs=4))
+        psum_mix = stack.enter_context(tc.psum_pool(name="psum_mix", bufs=1))
         psum_flip = stack.enter_context(tc.psum_pool(name="psum_flip", bufs=2))
         psum_score = stack.enter_context(tc.psum_pool(name="psum_score", bufs=1))
         stack.enter_context(tc.manual_schedule())
@@ -97,6 +100,8 @@ def tile_unitagcn_pa_t_kernel(tc, x, A, PA, Wa, Wb, out):
 
         ident = consts.tile([P, P], F32)
         make_identity(nc, ident[:])
+        ident_bf16 = consts.tile([P, P], BF16)
+        make_identity(nc, ident_bf16[:])
         adjacency = consts.tile([P, S, V], F32)
         nc.gpsimd.tensor_tensor(out=adjacency[:], in0=a_rows[:], in1=pa_rows[:], op=ALU.add)
 
@@ -146,10 +151,33 @@ def tile_unitagcn_pa_t_kernel(tc, x, A, PA, Wa, Wb, out):
             share = LAST_SCALAR_COLS if k == STEPS - 1 else SCALAR_COLS
             return BLOCK - (min(share, BLOCK) if h == 1 else max(share - BLOCK, 0))
 
+        mixed = {}
+
+        def mix(k):
+            bank = psum_mix.tile([P, MIX_COLS * PACK], BF16, name="mix")
+            for first in range(0, MIX_COLS, MIX_RUN):
+                column = BLOCK - MIX_COLS + first
+                nc.tensor.matmul(
+                    bank[:, first * PACK : (first + MIX_RUN) * PACK].rearrange(
+                        "p (c i j) -> p c j i", i=4, j=PACK
+                    ),
+                    lhsT=ident_bf16[:],
+                    rhs=raws[k][1][:, :, column : column + MIX_RUN].rearrange(
+                        "p j (c i) -> p c j i", i=4
+                    ),
+                    start=True,
+                    stop=True,
+                )
+            mixed[k] = bank
+
         def regroup_on_scalar(k):
             for h in range(C_PASSES):
-                if vector_cols(k, h) < BLOCK:
-                    regroup(nc.scalar.copy, k, h, vector_cols(k, h), BLOCK)
+                last = BLOCK - MIX_COLS if h == 1 else BLOCK
+                if vector_cols(k, h) < last:
+                    regroup(nc.scalar.copy, k, h, vector_cols(k, h), last)
+            nc.scalar.copy(
+                out=groups[k][1][:, (BLOCK - MIX_COLS) * PACK :], in_=mixed[k][:]
+            )
 
         def regroup_on_vector(k):
             for h in range(C_PASSES):
@@ -360,6 +388,7 @@ def tile_unitagcn_pa_t_kernel(tc, x, A, PA, Wa, Wb, out):
             if half == 0:
                 quantise_weights()
             project(0, half_banks[half])
+        mix(1)
         empty_banks(0, half_banks[0], only_scalar)
         regroup_on_scalar(1)
         empty_banks(0, half_banks[1], only_scalar)
@@ -372,6 +401,7 @@ def tile_unitagcn_pa_t_kernel(tc, x, A, PA, Wa, Wb, out):
                     flip_back(n, every, psum_score, "score")
             regroup_on_vector(k)
             if k + 1 < STEPS:
+                mix(k + 1)
                 regroup_on_scalar(k + 1)
             for n in range(N - 1):
                 if k == scored(n) + 1:

@@ -52,8 +52,7 @@ def tile_unitagcn_pa_t_kernel(tc, x, A, PA, Wa, Wb, out):
         rows_pool = stack.enter_context(tc.tile_pool(name="rows", bufs=2))
         f_pool = stack.enter_context(tc.tile_pool(name="f", bufs=2))
         soft_pool = stack.enter_context(tc.tile_pool(name="soft", bufs=3))
-        psum_proj = stack.enter_context(tc.psum_pool(name="psum_proj", bufs=4))
-        psum_mix = stack.enter_context(tc.psum_pool(name="psum_mix", bufs=1))
+        psum_proj = stack.enter_context(tc.psum_pool(name="psum_proj", bufs=5))
         psum_flip = stack.enter_context(tc.psum_pool(name="psum_flip", bufs=2))
         psum_score = stack.enter_context(tc.psum_pool(name="psum_score", bufs=1))
         stack.enter_context(tc.manual_schedule())
@@ -154,7 +153,7 @@ def tile_unitagcn_pa_t_kernel(tc, x, A, PA, Wa, Wb, out):
         mixed = {}
 
         def mix(k):
-            bank = psum_mix.tile([P, MIX_COLS * PACK], BF16, name="mix")
+            bank = psum_flip.tile([P, MIX_COLS * PACK], BF16, name="mix", tag="flip")
             for first in range(0, MIX_COLS, MIX_RUN):
                 column = BLOCK - MIX_COLS + first
                 nc.tensor.matmul(
@@ -439,32 +438,32 @@ def tile_unitagcn_pa_t_kernel(tc, x, A, PA, Wa, Wb, out):
         for half in range(2):
             quantise_half(STEPS - 1, half)
             project(STEPS - 1, half_banks[half])
-        empty_banks(STEPS - 1, half_banks[0], [nc.vector.tensor_copy])
-        empty_banks(STEPS - 1, half_banks[1], only_scalar)
+        empty_banks(STEPS - 1, all_banks[:-1], [nc.vector.tensor_copy])
+        empty_banks(STEPS - 1, all_banks[-1:], only_scalar)
+        for part in (0, 2):
+            flip(last, part, psum_proj, "bank")
         for part in parts[2:]:
             quantise_f(before, part)
         score(before, every, psum_score, "score")
-        find_top(before, every)
         for part in (0, 2):
-            flip(last, part, psum_proj, "bank")
             empty_flips(last, part, only_scalar)
-        exponentiate(before, every)
-        for part in (0, 2):
             quantise_f(last, part)
+        find_top(before, every)
         for part in (1, 3):
             flip(last, part, psum_proj, "bank")
             empty_flips(last, part, only_scalar)
         score(last, halves[0], psum_flip, "flip")
-        normalise(before, every)
+        exponentiate(before, every)
+        quantise_f(last, 1)
         find_top(last, halves[0])
         exponentiate(last, halves[0])
-        for part in (1, 3):
-            quantise_f(last, part)
+        quantise_f(last, 3)
         score(last, halves[1], psum_flip, "flip")
+        normalise(before, every)
         flip_back(before, every, psum_score, "score")
-        normalise(last, halves[0])
         find_top(last, halves[1])
         exponentiate(last, halves[1])
+        normalise(last, halves[0])
         flip_back(last, halves[0], psum_proj, "bank")
         add_and_store(before, every)
         normalise(last, halves[1])

@@ -34,8 +34,8 @@ BANKS = FRAMES // PAIR
 STEPS = N * BLOCKS
 AHEAD = 2
 PIECE = BLOCK // 4
-SCALAR_COLS = 704
-LAST_SCALAR_COLS = 896
+SCALAR_COLS = 640
+LAST_SCALAR_COLS = 832
 MIX_COLS = 256
 MIX_RUN = 128
 
@@ -83,26 +83,21 @@ def tile_unitagcn_pa_t_kernel(tc, x, A, PA, Wa, Wb, out):
                 load(k, h)
 
         w_rows = consts.tile([P, SIDES * C], BF16)
-        nc.scalar.dma_start(out=w_rows[:, 0:C], in_=Wa.rearrange("s i c -> (s i) c"))
-        nc.scalar.dma_start(out=w_rows[:, C : 2 * C], in_=Wb.rearrange("s i c -> (s i) c"))
         allocate(0)
         for half in range(2):
             for h in range(C_PASSES):
                 for piece in range(2 * half, 2 * half + 2):
                     load(0, h, piece * PIECE, (piece + 1) * PIECE)
+            if half == 0:
+                nc.sync.dma_start(out=w_rows[:, 0:C], in_=Wa.rearrange("s i c -> (s i) c"))
+                nc.sync.dma_start(out=w_rows[:, C : 2 * C], in_=Wb.rearrange("s i c -> (s i) c"))
         for k in range(1, AHEAD):
             load_block(k)
-        a_rows = consts.tile([P, S, V], BF16)
-        pa_rows = consts.tile([P, S, V], BF16)
-        nc.scalar.dma_start(out=a_rows[:], in_=A.rearrange("s v w -> v s w"))
-        nc.scalar.dma_start(out=pa_rows[:], in_=PA.rearrange("s v w -> v s w"))
 
         ident = consts.tile([P, P], F32)
         make_identity(nc, ident[:])
         ident_bf16 = consts.tile([P, P], BF16)
         make_identity(nc, ident_bf16[:])
-        adjacency = consts.tile([P, S, V], F32)
-        nc.gpsimd.tensor_tensor(out=adjacency[:], in0=a_rows[:], in1=pa_rows[:], op=ALU.add)
 
         w_words = w_rows[:].bitcast(F32).rearrange("p (a c) -> p a c", a=SIDES)
         w_grouped = consts.tile([P, C_PASSES * SIDES * SIDE_ROWS * PACK], BF16, align_bytes=64)
@@ -375,6 +370,13 @@ def tile_unitagcn_pa_t_kernel(tc, x, A, PA, Wa, Wb, out):
             return first(n) + len(parts)
 
         load_block(AHEAD)
+        a_rows = consts.tile([P, S, V], BF16)
+        pa_rows = consts.tile([P, S, V], BF16)
+        nc.sync.dma_start(out=a_rows[:], in_=A.rearrange("s v w -> v s w"))
+        nc.sync.dma_start(out=pa_rows[:], in_=PA.rearrange("s v w -> v s w"))
+
+        adjacency = consts.tile([P, S, V], F32)
+
         for half in range(2):
             left, middle, right = (column + half * BLOCK // 2 for column in (0, PIECE, 2 * PIECE))
             regroup(nc.scalar.copy, 0, 1, left, middle)
@@ -383,10 +385,11 @@ def tile_unitagcn_pa_t_kernel(tc, x, A, PA, Wa, Wb, out):
             regroup(nc.vector.tensor_copy, 0, 1, middle, right)
             if half == 0:
                 regroup_weights()
-            quantise_half(0, half)
-            if half == 0:
+            else:
                 quantise_weights()
-            project(0, half_banks[half])
+                project(0, half_banks[0])
+            quantise_half(0, half)
+        project(0, half_banks[1])
         mix(1)
         empty_banks(0, half_banks[0], only_scalar)
         regroup_on_scalar(1)
@@ -428,6 +431,8 @@ def tile_unitagcn_pa_t_kernel(tc, x, A, PA, Wa, Wb, out):
                 for n in range(N - 1):
                     if k == scored(n):
                         find_top(n, every)
+            if k == AHEAD:
+                nc.vector.tensor_tensor(out=adjacency[:], in0=a_rows[:], in1=pa_rows[:], op=ALU.add)
             for n in range(N - 1):
                 if k == scored(n) + 1:
                     normalise(n, every)

@@ -34,9 +34,10 @@ BANKS = FRAMES // PAIR
 STEPS = N * BLOCKS
 AHEAD = 2
 PIECE = BLOCK // 4
-SCALAR_COLS = 640
-LAST_SCALAR_COLS = 832
-MIX_COLS = 256
+SCALAR_COLS = 832
+LAST_SCALAR_COLS = 1024
+MIX_COLS = 448
+MIX_BANK = 256
 MIX_RUN = 128
 
 FLOPS = 2 * SIDES * SIDE_ROWS * C * N * T * V + 2 * N * S * V * V * KT
@@ -148,30 +149,33 @@ def tile_unitagcn_pa_t_kernel(tc, x, A, PA, Wa, Wb, out):
         mixed = {}
 
         def mix(k):
-            bank = psum_flip.tile([P, MIX_COLS * PACK], BF16, name="mix", tag="flip")
-            for first in range(0, MIX_COLS, MIX_RUN):
-                column = BLOCK - MIX_COLS + first
-                nc.tensor.matmul(
-                    bank[:, first * PACK : (first + MIX_RUN) * PACK].rearrange(
-                        "p (c i j) -> p c j i", i=4, j=PACK
-                    ),
-                    lhsT=ident_bf16[:],
-                    rhs=raws[k][1][:, :, column : column + MIX_RUN].rearrange(
-                        "p j (c i) -> p c j i", i=4
-                    ),
-                    start=True,
-                    stop=True,
-                )
-            mixed[k] = bank
+            for begin in range(BLOCK - MIX_COLS, BLOCK, MIX_BANK):
+                end = min(begin + MIX_BANK, BLOCK)
+                bank = psum_flip.tile([P, MIX_BANK * PACK], BF16, name="mix", tag="flip")
+                for first in range(begin, end, MIX_RUN):
+                    last = min(first + MIX_RUN, end)
+                    nc.tensor.matmul(
+                        bank[:, (first - begin) * PACK : (last - begin) * PACK].rearrange(
+                            "p (c i j) -> p c j i", i=4, j=PACK
+                        ),
+                        lhsT=ident_bf16[:],
+                        rhs=raws[k][1][:, :, first:last].rearrange("p j (c i) -> p c j i", i=4),
+                        start=True,
+                        stop=True,
+                    )
+                mixed[k, begin] = (bank, end)
 
         def regroup_on_scalar(k):
             for h in range(C_PASSES):
                 last = BLOCK - MIX_COLS if h == 1 else BLOCK
                 if vector_cols(k, h) < last:
                     regroup(nc.scalar.copy, k, h, vector_cols(k, h), last)
-            nc.scalar.copy(
-                out=groups[k][1][:, (BLOCK - MIX_COLS) * PACK :], in_=mixed[k][:]
-            )
+            for begin in range(BLOCK - MIX_COLS, BLOCK, MIX_BANK):
+                bank, end = mixed[k, begin]
+                nc.scalar.copy(
+                    out=groups[k][1][:, begin * PACK : end * PACK],
+                    in_=bank[:, : (end - begin) * PACK],
+                )
 
         def regroup_on_vector(k):
             for h in range(C_PASSES):

@@ -34,9 +34,9 @@ BANKS = FRAMES // PAIR
 STEPS = N * BLOCKS
 AHEAD = 2
 PIECE = BLOCK // 4
-SCALAR_COLS = 832
-LAST_SCALAR_COLS = 1024
-MIX_COLS = 448
+SCALAR_COLS = 704
+LAST_SCALAR_COLS = 896
+MIX_COLS = 384
 MIX_BANK = 256
 MIX_RUN = 128
 
@@ -405,10 +405,13 @@ def tile_unitagcn_pa_t_kernel(tc, x, A, PA, Wa, Wb, out):
             for n in range(N - 1):
                 if k == scored(n) + 2:
                     flip_back(n, every, psum_score, "score")
+            due = [(n, part) for n in range(N - 1) for part in parts if k == flipped(n, part)]
+            for n, part in due[1:]:
+                flip(n, part, psum_flip, "flip")
+                empty_flips(n, part, only_scalar)
+            if k > 1:
+                empty_banks(k - 1, all_banks, only_scalar)
             regroup_on_vector(k)
-            if k + 1 < STEPS:
-                mix(k + 1)
-                regroup_on_scalar(k + 1)
             for n in range(N - 1):
                 if k == scored(n) + 1:
                     exponentiate(n, every)
@@ -420,15 +423,12 @@ def tile_unitagcn_pa_t_kernel(tc, x, A, PA, Wa, Wb, out):
                         quantise_f(n, part)
                 if k == scored(n):
                     score(n, every, psum_score, "score")
-            due = [(n, part) for n in range(N - 1) for part in parts if k == flipped(n, part)]
-            for n, part in due[1:]:
-                flip(n, part, psum_flip, "flip")
-                empty_flips(n, part, only_scalar)
-            if k > 1:
-                empty_banks(k - 1, all_banks, only_scalar)
             for n, part in due[:1]:
                 flip(n, part, psum_flip, "flip")
                 empty_flips(n, part, only_scalar)
+            if k + 1 < STEPS:
+                mix(k + 1)
+                regroup_on_scalar(k + 1)
             if k < STEPS - 1:
                 quantise_x(k, 1)
                 project(k, all_banks)

@@ -34,8 +34,8 @@ BANKS = FRAMES // PAIR
 STEPS = N * BLOCKS
 AHEAD = 2
 PIECE = BLOCK // 4
-SCALAR_COLS = 704
-LAST_SCALAR_COLS = 896
+SCALAR_COLS = 768
+LAST_SCALAR_COLS = 960
 MIX_COLS = 384
 MIX_BANK = 256
 MIX_RUN = 128
@@ -417,15 +417,15 @@ def tile_unitagcn_pa_t_kernel(tc, x, A, PA, Wa, Wb, out):
                     exponentiate(n, every)
             if k < STEPS - 1:
                 quantise_x(k, 0)
+            for n, part in due[:1]:
+                flip(n, part, psum_flip, "flip")
+                empty_flips(n, part, only_scalar)
             for n in range(N - 1):
                 for part in parts:
                     if k == flipped(n, part) + 1:
                         quantise_f(n, part)
                 if k == scored(n):
                     score(n, every, psum_score, "score")
-            for n, part in due[:1]:
-                flip(n, part, psum_flip, "flip")
-                empty_flips(n, part, only_scalar)
             if k + 1 < STEPS:
                 mix(k + 1)
                 regroup_on_scalar(k + 1)

@@ -34,8 +34,9 @@ BANKS = FRAMES // PAIR
 STEPS = N * BLOCKS
 AHEAD = 2
 PIECE = BLOCK // 4
-SCALAR_COLS = 768
-LAST_SCALAR_COLS = 960
+SCALAR_COLS = 752
+FIRST_SCALAR_COLS = 624
+LAST_SCALAR_COLS = 1024
 MIX_COLS = 384
 MIX_BANK = 256
 MIX_RUN = 128
@@ -143,7 +144,7 @@ def tile_unitagcn_pa_t_kernel(tc, x, A, PA, Wa, Wb, out):
             )
 
         def vector_cols(k, h):
-            share = LAST_SCALAR_COLS if k == STEPS - 1 else SCALAR_COLS
+            share = {1: FIRST_SCALAR_COLS, STEPS - 1: LAST_SCALAR_COLS}.get(k, SCALAR_COLS)
             return BLOCK - (min(share, BLOCK) if h == 1 else max(share - BLOCK, 0))
 
         mixed = {}
@@ -334,12 +335,14 @@ def tile_unitagcn_pa_t_kernel(tc, x, A, PA, Wa, Wb, out):
             inverse = soft_pool.tile([P, len(run)], F32)
             nc.vector.reciprocal(out=inverse[:], in_=state["sums"][:])
             attn = soft_pool.tile([P, len(run), V], F32)
-            nc.vector.tensor_tensor(
-                out=attn[:],
-                in0=state["expd"][:],
-                in1=inverse[:].unsqueeze(2).to_broadcast([P, len(run), V]),
-                op=ALU.mult,
-            )
+            for r in range(len(run)):
+                nc.vector.tensor_scalar(
+                    out=attn[:, r, :],
+                    in0=state["expd"][:, r, :],
+                    scalar1=inverse[:, r : r + 1],
+                    scalar2=None,
+                    op0=ALU.mult,
+                )
             state["attn"] = attn
 
         def flip_back(n, run, pool, tag):
@@ -415,15 +418,16 @@ def tile_unitagcn_pa_t_kernel(tc, x, A, PA, Wa, Wb, out):
             for n in range(N - 1):
                 if k == scored(n) + 1:
                     exponentiate(n, every)
+            for n in range(N - 1):
+                for part in parts:
+                    if k == flipped(n, part) + 1:
+                        quantise_f(n, part)
             if k < STEPS - 1:
                 quantise_x(k, 0)
             for n, part in due[:1]:
                 flip(n, part, psum_flip, "flip")
                 empty_flips(n, part, only_scalar)
             for n in range(N - 1):
-                for part in parts:
-                    if k == flipped(n, part) + 1:
-                        quantise_f(n, part)
                 if k == scored(n):
                     score(n, every, psum_score, "score")
             if k + 1 < STEPS:

from contextlib import ExitStack

import concourse.mybir as mybir
from concourse.masks import make_identity

F32 = mybir.dt.float32
BF16 = mybir.dt.bfloat16
U32 = mybir.dt.uint32
U8 = mybir.dt.uint8
FP8X4 = mybir.dt.float8_e4m3fn_x4
ALU = mybir.AluOpType
ACT = mybir.ActivationFunctionType

N, C, T, V, S, INTER = 4, 1024, 32, 128, 4, 32
KT = INTER * T

P = 128
PACK = 4
PAIRS = PACK // 2
K_PASS = P * PACK
C_PASSES = C // K_PASS
KT_PASSES = KT // K_PASS

SIDES = 2
SIDE_ROWS = S * INTER
OPERANDS = SIDES * S
WORDS = T // PACK

BLOCK = 1024
BLOCKS = T * V // BLOCK
FRAMES = BLOCK // V
PAIR = 2
BANKS = FRAMES // PAIR
STEPS = N * BLOCKS
AHEAD = 2
PIECE = BLOCK // 4
SCALAR_COLS = 752
FIRST_SCALAR_COLS = 624
LAST_SCALAR_COLS = 1024
MIX_COLS = 384
MIX_BANK = 256
MIX_RUN = 128

FLOPS = 2 * SIDES * SIDE_ROWS * C * N * T * V + 2 * N * S * V * V * KT


def tile_unitagcn_pa_t_kernel(tc, x, A, PA, Wa, Wb, out):
    nc = tc.nc
    with ExitStack() as stack:
        consts = stack.enter_context(tc.tile_pool(name="consts", bufs=1))
        raw_pool = stack.enter_context(tc.tile_pool(name="raw", bufs=C_PASSES * (AHEAD + 1)))
        grouped_pool = stack.enter_context(tc.tile_pool(name="grouped", bufs=C_PASSES * 3))
        xq_pool = stack.enter_context(tc.tile_pool(name="xq", bufs=3))
        rows_pool = stack.enter_context(tc.tile_pool(name="rows", bufs=2))
        f_pool = stack.enter_context(tc.tile_pool(name="f", bufs=2))
        soft_pool = stack.enter_context(tc.tile_pool(name="soft", bufs=3))
        psum_proj = stack.enter_context(tc.psum_pool(name="psum_proj", bufs=5))
        psum_flip = stack.enter_context(tc.psum_pool(name="psum_flip", bufs=2))
        psum_score = stack.enter_context(tc.psum_pool(name="psum_score", bufs=1))
        stack.enter_context(tc.manual_schedule())

        raws = {}
        groups = {}

        def allocate(k):
            raws[k] = [
                raw_pool.tile([P, PACK, BLOCK], BF16, name="raw") for h in range(C_PASSES)
            ]
            groups[k] = [
                grouped_pool.tile([P, BLOCK * PACK], BF16, align_bytes=64, name="grouped")
                for h in range(C_PASSES)
            ]

        def load(k, h, first=0, last=BLOCK):
            n, part = divmod(k, BLOCKS)
            x_rows = x[n].rearrange("(h p j) t v -> h p j (t v)", h=C_PASSES, p=P, j=PACK)
            nc.sync.dma_start(
                out=raws[k][h][:, :, first:last],
                in_=x_rows[h][:, :, part * BLOCK + first : part * BLOCK + last],
            )

        def load_block(k):
            allocate(k)
            for h in range(C_PASSES):
                load(k, h)

        w_rows = consts.tile([P, SIDES * C], BF16)
        allocate(0)
        for half in range(2):
            for h in range(C_PASSES):
                for piece in range(2 * half, 2 * half + 2):
                    load(0, h, piece * PIECE, (piece + 1) * PIECE)
            if half == 0:
                nc.sync.dma_start(out=w_rows[:, 0:C], in_=Wa.rearrange("s i c -> (s i) c"))
                nc.sync.dma_start(out=w_rows[:, C : 2 * C], in_=Wb.rearrange("s i c -> (s i) c"))
        for k in range(1, AHEAD):
            load_block(k)

        ident = consts.tile([P, P], F32)
        make_identity(nc, ident[:])
        ident_bf16 = consts.tile([P, P], BF16)
        make_identity(nc, ident_bf16[:])

        w_words = w_rows[:].bitcast(F32).rearrange("p (a c) -> p a c", a=SIDES)
        w_grouped = consts.tile([P, C_PASSES * SIDES * SIDE_ROWS * PACK], BF16, align_bytes=64)
        w_grouped_words = w_grouped[:].bitcast(F32).rearrange(
            "p (h i s a u) -> p h s i a u", h=C_PASSES, i=INTER, s=S, a=SIDES, u=PAIRS
        )
        w_codes = consts.tile([P, C_PASSES, SIDES * SIDE_ROWS], U32, align_bytes=64)
        w_scales = consts.tile([P, C_PASSES, SIDES * SIDE_ROWS], U8, align_bytes=64)

        def regroup_weights():
            for h in range(C_PASSES):
                bank = psum_flip.tile([P, SIDES, PAIRS, SIDE_ROWS], F32, tag="flip")
                for a in range(SIDES):
                    for u in range(PAIRS):
                        first = h * (K_PASS // 2) + u
                        nc.tensor.transpose(
                            bank[:, a, u, :],
                            w_words[:, a, first : first + K_PASS // 2 - 1 : PAIRS],
                            ident[:],
                        )
                rows = bank[:].rearrange("p a u (s i) -> p s i a u", s=S)
                for s in range(S):
                    nc.scalar.copy(out=w_grouped_words[:, h, s], in_=rows[:, s])

        def quantise_weights():
            nc.vector.quantize_mx(
                out=w_codes[:].rearrange("p h r -> p (h r)").bitcast(FP8X4),
                scales=w_scales[:].rearrange("p h r -> p (h r)"),
                in_=w_grouped[:],
            )

        xq = {}
        banks = {}
        f_rows = {}

        def regroup(copy, k, h, first, last):
            copy(
                out=groups[k][h][:].rearrange("p (c j) -> p c j", j=PACK)[:, first:last].rearrange(
                    "p (c i) j -> p c j i", i=4
                ),
                in_=raws[k][h][:, :, first:last].rearrange("p j (c i) -> p c j i", i=4),
            )

        def vector_cols(k, h):
            share = {1: FIRST_SCALAR_COLS, STEPS - 1: LAST_SCALAR_COLS}.get(k, SCALAR_COLS)
            return BLOCK - (min(share, BLOCK) if h == 1 else max(share - BLOCK, 0))

        mixed = {}

        def mix(k):
            for begin in range(BLOCK - MIX_COLS, BLOCK, MIX_BANK):
                end = min(begin + MIX_BANK, BLOCK)
                bank = psum_flip.tile([P, MIX_BANK * PACK], BF16, name="mix", tag="flip")
                for first in range(begin, end, MIX_RUN):
                    last = min(first + MIX_RUN, end)
                    nc.tensor.matmul(
                        bank[:, (first - begin) * PACK : (last - begin) * PACK].rearrange(
                            "p (c i j) -> p c j i", i=4, j=PACK
                        ),
                        lhsT=ident_bf16[:],
                        rhs=raws[k][1][:, :, first:last].rearrange("p j (c i) -> p c j i", i=4),
                        start=True,
                        stop=True,
                    )
                mixed[k, begin] = (bank, end)

        def regroup_on_scalar(k):
            for h in range(C_PASSES):
                last = BLOCK - MIX_COLS if h == 1 else BLOCK
                if vector_cols(k, h) < last:
                    regroup(nc.scalar.copy, k, h, vector_cols(k, h), last)
            for begin in range(BLOCK - MIX_COLS, BLOCK, MIX_BANK):
                bank, end = mixed[k, begin]
                nc.scalar.copy(
                    out=groups[k][1][:, begin * PACK : end * PACK],
                    in_=bank[:, : (end - begin) * PACK],
                )

        def regroup_on_vector(k):
            for h in range(C_PASSES):
                if vector_cols(k, h) > 0:
                    regroup(nc.vector.tensor_copy, k, h, 0, vector_cols(k, h))

        def quantise_x(k, h, first=0, last=BLOCK):
            if k not in xq:
                codes = xq_pool.tile([P, C_PASSES, BLOCK], U32, align_bytes=64)
                scales = xq_pool.tile([P, C_PASSES, BLOCK], U8, align_bytes=64)
                xq[k] = (codes, scales)
            codes, scales = xq[k]
            nc.vector.quantize_mx(
                out=codes[:, h, first:last].bitcast(FP8X4),
                scales=scales[:, h, first:last],
                in_=groups[k][h][:, first * PACK : last * PACK],
            )

        def quantise_half(k, half):
            for h in range(C_PASSES):
                quantise_x(k, h, half * BLOCK // 2, (half + 1) * BLOCK // 2)

        all_banks = range(BANKS)
        half_banks = [range(0, BANKS // 2), range(BANKS // 2, BANKS)]

        def project(k, some_banks):
            codes, scales = xq[k]
            for pair in some_banks:
                bank = psum_proj.tile([P, PAIR, SIDES * SIDE_ROWS], F32, tag="bank")
                for e in range(PAIR):
                    frame = pair * PAIR + e
                    joints = slice(frame * V, (frame + 1) * V)
                    for h in range(C_PASSES):
                        nc.tensor.matmul_mx(
                            out=bank[:, e, :],
                            lhsT=codes[:, h, joints].bitcast(FP8X4),
                            lhsT_scale=scales[:, h, joints],
                            rhs=w_codes[:, h, :].bitcast(FP8X4),
                            rhs_scale=w_scales[:, h, :],
                            start=(h == 0),
                            stop=(h == C_PASSES - 1),
                        )
                banks[k, pair] = bank

        def empty_banks(k, some_banks, copies):
            n, part = divmod(k, BLOCKS)
            if n not in f_rows:
                f_rows[n] = rows_pool.tile([P, T * SIDES * SIDE_ROWS], BF16, name="f_rows")
            view = f_rows[n][:].rearrange(
                "p (u i t q e) -> p t u i q e", u=PAIRS, i=INTER, t=WORDS, q=OPERANDS, e=PAIR
            )
            for pair in some_banks:
                t_word, u = divmod(part * BANKS + pair, PAIRS)
                copies[pair % len(copies)](
                    out=view[:, t_word, u],
                    in_=banks[k, pair][:].rearrange("p e (i q) -> p i q e", q=OPERANDS),
                )

        flips = {}
        turned = {}
        fq = {}
        soft = {}
        every = range(S)
        halves = [range(0, S // 2), range(S // 2, S)]

        def flip(n, part, pool, tag):
            b, half = divmod(part, 2)
            words = f_rows[n][:].bitcast(F32)
            for s in halves[half]:
                bank = pool.tile([P, SIDES, PAIRS, V], F32, tag=tag)
                for a in range(SIDES):
                    for u in range(PAIRS):
                        first = (u * KT_PASSES + b) * P * OPERANDS + SIDES * s + a
                        nc.tensor.transpose(
                            bank[:, a, u, :],
                            words[:, first : first + (P - 1) * OPERANDS + 1 : OPERANDS],
                            ident[:],
                        )
                flips[n, b, s] = bank

        def empty_flips(n, part, copies):
            b, half = divmod(part, 2)
            if (n, b) not in turned:
                turned[n, b] = f_pool.tile(
                    [P, OPERANDS * V * PACK], BF16, align_bytes=64, name="turned"
                )
            view = turned[n, b][:].bitcast(F32).rearrange(
                "p (s a v u) -> p s a v u", s=S, a=SIDES, v=V, u=PAIRS
            )
            for s in halves[half]:
                copies[s % len(copies)](
                    out=view[:, s], in_=flips[n, b, s][:].rearrange("p a u v -> p a v u")
                )

        def quantise_f(n, part):
            if n not in fq:
                codes = f_pool.tile([P, KT_PASSES, OPERANDS * V], U32, align_bytes=64, name="f_codes")
                scales = f_pool.tile([P, KT_PASSES, OPERANDS * V], U8, align_bytes=64, name="f_scales")
                fq[n] = (codes, scales)
            codes, scales = fq[n]
            b, half = divmod(part, 2)
            cols = slice(halves[half].start * SIDES * V, halves[half].stop * SIDES * V)
            nc.vector.quantize_mx(
                out=codes[:, b, cols].bitcast(FP8X4),
                scales=scales[:, b, cols],
                in_=turned[n, b][:, cols.start * PACK : cols.stop * PACK],
            )

        def score(n, run, pool, tag):
            codes, scales = fq[n]
            scores = pool.tile([P, len(run), V], F32, name="scores", tag=tag)
            for r, s in enumerate(run):
                fa_cols = slice(SIDES * s * V, (SIDES * s + 1) * V)
                fb_cols = slice((SIDES * s + 1) * V, (SIDES * s + 2) * V)
                for b in range(KT_PASSES):
                    nc.tensor.matmul_mx(
                        out=scores[:, r, :],
                        lhsT=codes[:, b, fb_cols].bitcast(FP8X4),
                        lhsT_scale=scales[:, b, fb_cols],
                        rhs=codes[:, b, fa_cols].bitcast(FP8X4),
                        rhs_scale=scales[:, b, fa_cols],
                        start=(b == 0),
                        stop=(b == KT_PASSES - 1),
                    )
            soft[n, run.start] = {"scores": scores}

        def find_top(n, run):
            top = soft_pool.tile([P, len(run)], F32)
            state = soft[n, run.start]
            nc.vector.tensor_reduce(
                out=top[:], in_=state["scores"][:], axis=mybir.AxisListType.X, op=ALU.max
            )
            shift = soft_pool.tile([P, len(run)], F32)
            nc.vector.tensor_scalar(
                out=shift[:], in0=top[:], scalar1=-1.0 / KT, scalar2=None, op0=ALU.mult
            )
            state["shift"] = shift

        def exponentiate(n, run):
            state = soft[n, run.start]
            expd = soft_pool.tile([P, len(run), V], F32)
            sums = soft_pool.tile([P, len(run)], F32)
            for r in range(len(run)):
                nc.scalar.activation(
                    out=expd[:, r, :],
                    in_=state["scores"][:, r, :],
                    func=ACT.Exp,
                    bias=state["shift"][:, r : r + 1],
                    scale=1.0 / KT,
                    accum_out=sums[:, r : r + 1],
                )
            state["expd"], state["sums"] = expd, sums

        def normalise(n, run):
            state = soft[n, run.start]
            inverse = soft_pool.tile([P, len(run)], F32)
            nc.vector.reciprocal(out=inverse[:], in_=state["sums"][:])
            attn = soft_pool.tile([P, len(run), V], F32)
            for r in range(len(run)):
                nc.vector.tensor_scalar(
                    out=attn[:, r, :],
                    in0=state["expd"][:, r, :],
                    scalar1=inverse[:, r : r + 1],
                    scalar2=None,
                    op0=ALU.mult,
                )
            state["attn"] = attn

        def flip_back(n, run, pool, tag):
            state = soft[n, run.start]
            flipped = pool.tile([P, len(run), V], F32, name="flipped", tag=tag)
            for r in range(len(run)):
                nc.tensor.transpose(flipped[:, r, :], state["attn"][:, r, :], ident[:])
            state["flipped"] = flipped

        def add_and_store(n, run):
            result = soft_pool.tile([P, len(run), V], F32)
            nc.vector.tensor_tensor(
                out=result[:],
                in0=soft[n, run.start]["flipped"][:],
                in1=adjacency[:, run.start : run.stop, :],
                op=ALU.add,
            )
            nc.sync.dma_start(
                out=out[n, run.start : run.stop].rearrange("s v w -> v s w"), in_=result[:]
            )

        only_scalar = [nc.scalar.copy]
        parts = range(2 * KT_PASSES)

        def first(n):
            return BLOCKS * (n + 1) + 1

        def flipped(n, part):
            return first(n) + (min(part, 2) if n == N - 2 else part)

        def scored(n):
            return first(n) + len(parts)

        load_block(AHEAD)
        a_rows = consts.tile([P, S, V], BF16)
        pa_rows = consts.tile([P, S, V], BF16)
        nc.sync.dma_start(out=a_rows[:], in_=A.rearrange("s v w -> v s w"))
        nc.sync.dma_start(out=pa_rows[:], in_=PA.rearrange("s v w -> v s w"))

        adjacency = consts.tile([P, S, V], F32)

        for half in range(2):
            left, middle, right = (column + half * BLOCK // 2 for column in (0, PIECE, 2 * PIECE))
            regroup(nc.scalar.copy, 0, 1, left, middle)
            for piece in (left, middle):
                regroup(nc.vector.tensor_copy, 0, 0, piece, piece + PIECE)
            regroup(nc.vector.tensor_copy, 0, 1, middle, right)
            if half == 0:
                regroup_weights()
            else:
                quantise_weights()
                project(0, half_banks[0])
            quantise_half(0, half)
        project(0, half_banks[1])
        mix(1)
        empty_banks(0, half_banks[0], only_scalar)
        regroup_on_scalar(1)
        empty_banks(0, half_banks[1], only_scalar)

        for k in range(1, STEPS):
            if k + AHEAD < STEPS:
                load_block(k + AHEAD)
            for n in range(N - 1):
                if k == scored(n) + 2:
                    flip_back(n, every, psum_score, "score")
            due = [(n, part) for n in range(N - 1) for part in parts if k == flipped(n, part)]
            for n, part in due[1:]:
                flip(n, part, psum_flip, "flip")
                empty_flips(n, part, only_scalar)
            if k > 1:
                empty_banks(k - 1, all_banks, only_scalar)
            regroup_on_vector(k)
            for n in range(N - 1):
                if k == scored(n) + 1:
                    exponentiate(n, every)
            for n in range(N - 1):
                for part in parts:
                    if k == flipped(n, part) + 1:
                        quantise_f(n, part)
            if k < STEPS - 1:
                quantise_x(k, 0)
            for n, part in due[:1]:
                flip(n, part, psum_flip, "flip")
                empty_flips(n, part, only_scalar)
            for n in range(N - 1):
                if k == scored(n):
                    score(n, every, psum_score, "score")
            if k + 1 < STEPS:
                mix(k + 1)
                regroup_on_scalar(k + 1)
            if k < STEPS - 1:
                quantise_x(k, 1)
                project(k, all_banks)
                for n in range(N - 1):
                    if k == scored(n):
                        find_top(n, every)
            if k == AHEAD:
                nc.vector.tensor_tensor(out=adjacency[:], in0=a_rows[:], in1=pa_rows[:], op=ALU.add)
            for n in range(N - 1):
                if k == scored(n) + 1:
                    normalise(n, every)
                if k == scored(n) + 2:
                    add_and_store(n, every)

        before, last = N - 2, N - 1
        for half in range(2):
            quantise_half(STEPS - 1, half)
            project(STEPS - 1, half_banks[half])
        empty_banks(STEPS - 1, all_banks[:-1], [nc.vector.tensor_copy])
        empty_banks(STEPS - 1, all_banks[-1:], only_scalar)
        for part in (0, 2):
            flip(last, part, psum_proj, "bank")
        for part in parts[2:]:
            quantise_f(before, part)
        score(before, every, psum_score, "score")
        for part in (0, 2):
            empty_flips(last, part, only_scalar)
            quantise_f(last, part)
        find_top(before, every)
        for part in (1, 3):
            flip(last, part, psum_proj, "bank")
            empty_flips(last, part, only_scalar)
        score(last, halves[0], psum_flip, "flip")
        exponentiate(before, every)
        quantise_f(last, 1)
        find_top(last, halves[0])
        exponentiate(last, halves[0])
        quantise_f(last, 3)
        score(last, halves[1], psum_flip, "flip")
        normalise(before, every)
        flip_back(before, every, psum_score, "score")
        find_top(last, halves[1])
        exponentiate(last, halves[1])
        normalise(last, halves[0])
        flip_back(last, halves[0], psum_proj, "bank")
        add_and_store(before, every)
        normalise(last, halves[1])
        add_and_store(last, halves[0])
        flip_back(last, halves[1], psum_proj, "bank")
        add_and_store(last, halves[1])
